import numpy as np
import ml_dtypes


def mxq(x, axis, fmt="e4m3"):
    dtype, down = {"e4m3": (ml_dtypes.float8_e4m3fn, 7), "e5m2": (ml_dtypes.float8_e5m2, 14)}[fmt]
    v = np.moveaxis(np.asarray(x, np.float32).astype(ml_dtypes.bfloat16).astype(np.float64), axis, -1)
    blocks = v.reshape(v.shape[:-1] + (-1, 32))
    amax = np.abs(blocks).max(-1, keepdims=True)
    byte = np.maximum(np.where(amax > 0, np.frexp(amax)[1] - 1 + 127, 0) - down, 1)
    scale = np.exp2(byte - 127.0)
    codes = (blocks / scale).astype(np.float32).astype(dtype).astype(np.float64)
    return np.moveaxis((codes * scale).reshape(v.shape), -1, axis)


WIDE = False


def mx_kscale(k):
    if not WIDE:
        return np.ones(k)
    levels = np.array([10, -10, 5, -5, 0])
    a = np.random.permutation(np.resize(levels, k // 512 * 4)).reshape(k // 512, 4)
    idx = np.arange(k)
    return np.exp2(a[idx // 512, idx % 128 // 32])


BF16 = ml_dtypes.bfloat16


def bf(x):
    return np.asarray(x, np.float32).astype(BF16)


def f64(x):
    return np.asarray(x).astype(np.float64)


B, C, HH, WW, NH, HD, F = 16, 1024, 16, 16, 8, 32, 2048
E = NH * HD
EPS = 1e-5


def layer_norm(v, w, b):
    mu = v.mean(-1, keepdims=True)
    var = ((v - mu) ** 2).mean(-1, keepdims=True)
    return (v - mu) * (1.0 / np.sqrt(var + EPS)) * w + b


def draw_w(s):
    return bf((np.random.standard_normal((C, E)) * 2.0 / np.sqrt(C) / s[:, None]).reshape(NH, C, HD))


def setup_inputs():
    s = mx_kscale(C)
    return {"x": bf(np.random.standard_normal((B, C, HH, WW))),
            "ln1_w": bf((1.0 + 0.1 * np.random.standard_normal(C)) * s),
            "ln1_b": bf(0.1 * np.random.standard_normal(C) * s),
            "scale_norm1": bf(0.5 * (1.0 + 0.1 * np.random.standard_normal(1))),
            "W_Q": draw_w(s), "W_K": draw_w(s), "W_V": draw_w(s)}


def reference(x, ln1_w, ln1_b, scale_norm1, W_Q, W_K, W_V):
    xl = f64(x).transpose(0, 2, 3, 1)
    xn = layer_norm(xl, f64(ln1_w), f64(ln1_b)) * f64(scale_norm1)
    xq = mxq(xn, 3, "e4m3")
    q = (xq @ mxq(f64(W_Q).reshape(C, E), 0, "e4m3")).reshape(B, HH, WW, NH, HD)
    k = (xq @ mxq(f64(W_K).reshape(C, E), 0, "e4m3")).reshape(B, HH, WW, NH, HD)
    v = (xq @ mxq(f64(W_V).reshape(C, E), 0, "e4m3")).reshape(B, HH, WW, NH, HD)
    return q, k, v

@@ -1,0 +1,268 @@
+from contextlib import ExitStack
+
+import concourse.mybir as mybir
+from concourse.masks import make_identity
+
+BF16 = mybir.dt.bfloat16
+F32 = mybir.dt.float32
+U32 = mybir.dt.uint32
+U8 = mybir.dt.uint8
+FP8X4 = mybir.dt.float8_e4m3fn_x4
+ACT = mybir.ActivationFunctionType
+ALU = mybir.AluOpType
+
+P = 128
+PACK = 4
+K_PASS = P * PACK
+IMAGES = 16
+CHANNELS = 1024
+PIXELS = 256
+HEAD_COLS = 256
+PASSES = CHANNELS // K_PASS
+PLANES = PASSES * PACK
+TILES_PER_IMAGE = PIXELS // P
+TILES = IMAGES * TILES_PER_IMAGE
+GROUP_TILES = 4
+GROUP_PIXELS = GROUP_TILES * P
+PLANES_PER_SLOT = PLANES // GROUP_TILES
+OUT_COLS = 3 * HEAD_COLS
+QK_COLS = 2 * HEAD_COLS
+EPS = 1e-5
+
+MEASURE_LAG = 1
+CENTRE_LAG = 3
+UNFLIP_LAG = CENTRE_LAG + GROUP_TILES
+PROJECT_LAG = UNFLIP_LAG + GROUP_TILES
+WEIGHT_SLOT = 4
+EARLY_IMAGES = 4
+
+FLOPS = 2 * IMAGES * PIXELS * CHANNELS * OUT_COLS
+
+
+def tile_transformerconvblock_pa_t_kernel(
+    tc, x, ln1_w, ln1_b, scale_norm1, W_Q, W_K, W_V, out_0, out_1, out_2
+):
+    nc = tc.nc
+    weights = (W_Q, W_K, W_V)
+    outs = [o.rearrange("b h w a d -> (b h w) (a d)") for o in (out_0, out_1, out_2)]
+
+    with ExitStack() as stack:
+        stack.enter_context(tc.manual_schedule())
+        const = stack.enter_context(tc.tile_pool(name="const", bufs=1))
+        image_pool = stack.enter_context(tc.tile_pool(name="image_pool", bufs=IMAGES))
+        small = stack.enter_context(tc.tile_pool(name="small", bufs=4))
+        z_pool = stack.enter_context(tc.tile_pool(name="z_pool", bufs=2 * GROUP_TILES))
+        work = stack.enter_context(tc.tile_pool(name="work", bufs=2))
+        result_pool = stack.enter_context(tc.tile_pool(name="result_pool", bufs=4))
+        psum_fwd = stack.enter_context(tc.psum_pool(name="psum_fwd", bufs=4))
+        psum_back = stack.enter_context(tc.psum_pool(name="psum_back", bufs=2))
+        psum_acc = stack.enter_context(tc.psum_pool(name="psum_acc", bufs=1))
+
+        def load_image(b):
+            image = image_pool.tile([P, PASSES, PACK, PIXELS], BF16, name="image")
+            nc.sync.dma_start(
+                out=image[:].rearrange("p c t w -> p c (t w)"),
+                in_=x[b].rearrange("(c p t) h w -> p c (t h w)", c=PASSES, p=P),
+            )
+            return image
+
+        def load_weight(o):
+            w_raw = const.tile([P, PASSES, PACK, HEAD_COLS], BF16, name="w_raw%d" % o)
+            nc.sync.dma_start(
+                out=w_raw[:].rearrange("p c t n -> p c (t n)"),
+                in_=weights[o].rearrange("a r d -> (a r d)").rearrange("(c p tn) -> p c tn", c=PASSES, p=P),
+            )
+            return w_raw
+
+        images = [load_image(b) for b in range(EARLY_IMAGES)]
+        w_raws = [load_weight(o) for o in range(len(weights))]
+        images.extend([load_image(b) for b in range(EARLY_IMAGES, IMAGES)])
+
+        ident_bf16 = const.tile([P, P], BF16)
+        make_identity(nc, ident_bf16[:])
+        ident_f32 = const.tile([P, P], F32)
+        make_identity(nc, ident_f32[:])
+        eps = const.tile([P, 1], F32)
+        nc.vector.memset(eps[:], EPS)
+
+        gain_raw = const.tile([P, PASSES, PACK], BF16)
+        shift_raw = const.tile([P, PASSES, PACK], BF16)
+        mult_raw = const.tile([P, 1], BF16)
+        nc.scalar.dma_start(out=gain_raw[:], in_=ln1_w.rearrange("(c p t) -> p c t", c=PASSES, p=P))
+        nc.scalar.dma_start(out=shift_raw[:], in_=ln1_b.rearrange("(c p t) -> p c t", c=PASSES, p=P))
+        nc.scalar.dma_start(out=mult_raw[:], in_=scale_norm1.partition_broadcast(P))
+        mult = const.tile([P, 1], F32)
+        nc.vector.tensor_copy(out=mult[:], in_=mult_raw[:])
+        gain = const.tile([P, PLANES], F32)
+        shift = const.tile([P, PLANES], F32)
+        for scaled, raw in ((gain, gain_raw), (shift, shift_raw)):
+            nc.vector.tensor_scalar(
+                out=scaled[:], in0=raw[:].rearrange("p c t -> p (c t)"),
+                scalar1=mult[:, 0:1], scalar2=None, op0=ALU.mult,
+            )
+
+        w_grouped = const.tile([P, PASSES, OUT_COLS, PACK], BF16, align_bytes=64)
+        w_codes = const.tile([P, PASSES, OUT_COLS], U32, align_bytes=64)
+        w_scales = const.tile([P, PASSES, OUT_COLS], U8, align_bytes=64)
+
+        def regroup(dst, src):
+            nc.vector.tensor_copy(
+                out=dst.rearrange("p (w i) t -> p w t i", i=4), in_=src.rearrange("p t (w i) -> p w t i", i=4)
+            )
+
+        def quantise_weight(o):
+            cols = slice(o * HEAD_COLS, (o + 1) * HEAD_COLS)
+            for c in range(PASSES):
+                regroup(w_grouped[:, c, cols, :], w_raws[o][:, c])
+            for c in range(PASSES):
+                nc.vector.quantize_mx(
+                    out=w_codes[:, c, cols].bitcast(FP8X4),
+                    scales=w_scales[:, c, cols],
+                    in_=w_grouped[:, c, cols, :].rearrange("p n t -> p (n t)"),
+                )
+
+        x_t_of = {}
+        moments_of = {}
+        std_of = {}
+        affine_of = {}
+        z_of = {}
+        planes_of = {}
+        mx_of = {}
+        grouped_of = {}
+        acc_v_of = {}
+        result_of = {}
+
+        def flip(n):
+            image = images[n // TILES_PER_IMAGE]
+            pixels = slice((n % TILES_PER_IMAGE) * P, (n % TILES_PER_IMAGE + 1) * P)
+            x_t = psum_fwd.tile([P, PLANES, P], BF16, name="x_t")
+            for c in range(PASSES):
+                for t in range(PACK):
+                    nc.tensor.transpose(x_t[:, c * PACK + t, :], image[:, c, t, pixels], ident_bf16[:])
+            x_t_of[n] = x_t
+
+        def measure(n):
+            b, half = divmod(n, TILES_PER_IMAGE)
+            if half == 0:
+                moments_of[b] = small.tile([P, TILES_PER_IMAGE, 2], F32, name="moments")
+            stats = small.tile([P, PASSES, 6], F32, name="stats")
+            for c in range(PASSES):
+                nc.vector.bn_stats(out=stats[:, c, :], in_=x_t_of[n][:, c * PACK : (c + 1) * PACK, :])
+            nc.vector.bn_aggr(out=moments_of[b][:, half, :], in_=stats[:].rearrange("p c s -> p (c s)"))
+
+        def root(b):
+            std_of[b] = small.tile([P, TILES_PER_IMAGE], F32, name="std")
+            nc.scalar.activation(
+                out=std_of[b][:], in_=moments_of[b][:, :, 1], func=ACT.Sqrt, bias=eps[:, 0:1], scale=1.0
+            )
+
+        def invert(b):
+            rstd = small.tile([P, TILES_PER_IMAGE], F32, name="rstd")
+            nc.vector.reciprocal(out=rstd[:], in_=std_of.pop(b)[:])
+            offset = small.tile([P, TILES_PER_IMAGE], F32, name="offset")
+            nc.vector.scalar_tensor_tensor(
+                out=offset[:], in0=moments_of.pop(b)[:, :, 0], scalar=-1.0, in1=rstd[:], op0=ALU.mult, op1=ALU.mult
+            )
+            affine_of[b] = (rstd, offset)
+
+        def centre(n):
+            b, half = divmod(n, TILES_PER_IMAGE)
+            rstd, offset = affine_of[b]
+            z = z_pool.tile([P, CHANNELS], F32, name="z")
+            nc.scalar.activation(
+                out=z[:], in_=x_t_of.pop(n)[:].rearrange("p g j -> p (g j)"), func=ACT.Identity,
+                bias=offset[:, half : half + 1], scale=rstd[:, half : half + 1],
+            )
+            z_of[n] = z
+
+        def unflip(group, g):
+            if g == 0:
+                planes_of[group] = work.tile([P, PLANES, GROUP_PIXELS], BF16, name="planes")
+            z_t = psum_back.tile([P, GROUP_TILES, P], F32, name="z_t")
+            for m in range(GROUP_TILES):
+                nc.tensor.transpose(z_t[:, m, :], z_of[group * GROUP_TILES + m][:, g * P : (g + 1) * P], ident_f32[:])
+            nc.scalar.activation(
+                out=planes_of[group][:, g, :], in_=z_t[:].rearrange("p m j -> p (m j)"), func=ACT.Identity,
+                bias=shift[:, g : g + 1], scale=gain[:, g : g + 1],
+            )
+
+        def pack_words(group, c):
+            grouped = work.tile([P, GROUP_PIXELS, PACK], BF16, name="grouped", align_bytes=64)
+            regroup(grouped[:], planes_of[group][:, c * PACK : (c + 1) * PACK, :])
+            grouped_of[group, c] = grouped
+
+        def quantise(group, c):
+            if c == 0:
+                codes = work.tile([P, PASSES, GROUP_PIXELS], U32, name="codes", align_bytes=64)
+                scales = work.tile([P, PASSES, GROUP_PIXELS], U8, name="scales", align_bytes=64)
+                mx_of[group] = (codes, scales)
+            codes, scales = mx_of[group]
+            nc.vector.quantize_mx(
+                out=codes[:, c, :].bitcast(FP8X4),
+                scales=scales[:, c, :],
+                in_=grouped_of.pop((group, c))[:].rearrange("p w t -> p (w t)"),
+            )
+
+        def multiply(n):
+            b, half = divmod(n, TILES_PER_IMAGE)
+            codes, scales = mx_of[n // GROUP_TILES]
+            pixels = slice((n % GROUP_TILES) * P, (n % GROUP_TILES + 1) * P)
+            acc_qk = psum_acc.tile([P, QK_COLS], F32, name="acc_qk")
+            if half == 0:
+                acc_v_of[b] = psum_acc.tile([P, TILES_PER_IMAGE, HEAD_COLS], F32, name="acc_v")
+            for acc, cols in ((acc_qk[:], slice(0, QK_COLS)), (acc_v_of[b][:, half, :], slice(QK_COLS, OUT_COLS))):
+                for c in range(PASSES):
+                    nc.tensor.matmul_mx(
+                        out=acc,
+                        lhsT=codes[:, c, pixels].bitcast(FP8X4),
+                        lhsT_scale=scales[:, c, pixels],
+                        rhs=w_codes[:, c, cols].bitcast(FP8X4),
+                        rhs_scale=w_scales[:, c, cols],
+                        start=(c == 0),
+                        stop=(c == PASSES - 1),
+                    )
+            return acc_qk
+
+        def empty(n, acc_qk):
+            b, half = divmod(n, TILES_PER_IMAGE)
+            if half == 0:
+                result_of[b] = result_pool.tile([P, TILES_PER_IMAGE, OUT_COLS], F32, name="result")
+            result = result_of[b]
+            nc.vector.tensor_copy(out=result[:, half, 0:QK_COLS], in_=acc_qk[:])
+            if half == TILES_PER_IMAGE - 1:
+                nc.scalar.copy(out=result[:, :, QK_COLS:OUT_COLS], in_=acc_v_of.pop(b)[:])
+                for o, out in enumerate(outs):
+                    nc.sync.dma_start(
+                        out=out[b * PIXELS : (b + 1) * PIXELS, :].rearrange("(m p) n -> p m n", p=P),
+                        in_=result[:, :, o * HEAD_COLS : (o + 1) * HEAD_COLS],
+                    )
+
+        for slot in range(TILES + PROJECT_LAG):
+            measured = slot - MEASURE_LAG
+            centred = slot - CENTRE_LAG
+            unflipped = slot - UNFLIP_LAG
+            projected = slot - PROJECT_LAG
+
+            if 0 <= measured - 1 < TILES and (measured - 1) % TILES_PER_IMAGE == TILES_PER_IMAGE - 1:
+                invert((measured - 1) // TILES_PER_IMAGE)
+            if 0 <= unflipped < TILES:
+                group, quarter = divmod(unflipped, GROUP_TILES)
+                for g in range(quarter * PLANES_PER_SLOT, (quarter + 1) * PLANES_PER_SLOT):
+                    unflip(group, g)
+            if 0 <= measured < TILES:
+                measure(measured)
+            if 0 <= centred < TILES:
+                centre(centred)
+            pass_done = 0 <= unflipped < TILES and (unflipped + 1) % (GROUP_TILES // PASSES) == 0
+            if pass_done:
+                pack_words(unflipped // GROUP_TILES, (unflipped % GROUP_TILES) // (GROUP_TILES // PASSES))
+            if 0 <= projected < TILES:
+                empty(projected, multiply(projected))
+            if pass_done:
+                quantise(unflipped // GROUP_TILES, (unflipped % GROUP_TILES) // (GROUP_TILES // PASSES))
+            if 0 <= slot - WEIGHT_SLOT < len(weights):
+                quantise_weight(slot - WEIGHT_SLOT)
+            if slot < TILES:
+                flip(slot)
+            if 0 <= measured < TILES and measured % TILES_PER_IMAGE == TILES_PER_IMAGE - 1:
+                root(measured // TILES_PER_IMAGE)

@@ -230,7 +230,7 @@ def tile_transformerconvblock_pa_t_kernel(
             result = result_of[b]
             nc.vector.tensor_copy(out=result[:, half, 0:QK_COLS], in_=acc_qk[:])
             if half == TILES_PER_IMAGE - 1:
-                nc.scalar.copy(out=result[:, :, QK_COLS:OUT_COLS], in_=acc_v_of.pop(b)[:])
+                nc.vector.tensor_copy(out=result[:, :, QK_COLS:OUT_COLS], in_=acc_v_of.pop(b)[:])
                 for o, out in enumerate(outs):
                     nc.sync.dma_start(
                         out=out[b * PIXELS : (b + 1) * PIXELS, :].rearrange("(m p) n -> p m n", p=P),

@@ -30,9 +30,12 @@ QK_COLS = 2 * HEAD_COLS
 EPS = 1e-5
 
 MEASURE_LAG = 1
-CENTRE_LAG = 3
-UNFLIP_LAG = CENTRE_LAG + GROUP_TILES
-PROJECT_LAG = UNFLIP_LAG + GROUP_TILES
+CENTRE_LAG = 2
+TURN_BACK_LAG = CENTRE_LAG + GROUP_TILES
+GAIN_LAG = TURN_BACK_LAG + 1
+QUANTISE_LAG = GAIN_LAG + 1
+PROJECT_LAG = QUANTISE_LAG + GROUP_TILES - 1
+EMPTY_LAG = PROJECT_LAG + 1
 WEIGHT_SLOT = 4
 EARLY_IMAGES = 4
 
@@ -51,12 +54,13 @@ def tile_transformerconvblock_pa_t_kernel(
         const = stack.enter_context(tc.tile_pool(name="const", bufs=1))
         image_pool = stack.enter_context(tc.tile_pool(name="image_pool", bufs=IMAGES))
         small = stack.enter_context(tc.tile_pool(name="small", bufs=4))
-        z_pool = stack.enter_context(tc.tile_pool(name="z_pool", bufs=2 * GROUP_TILES))
+        z_pool = stack.enter_context(tc.tile_pool(name="z_pool", bufs=2 * GROUP_TILES + 2))
         work = stack.enter_context(tc.tile_pool(name="work", bufs=2))
         result_pool = stack.enter_context(tc.tile_pool(name="result_pool", bufs=4))
-        psum_fwd = stack.enter_context(tc.psum_pool(name="psum_fwd", bufs=4))
+        psum_fwd = stack.enter_context(tc.psum_pool(name="psum_fwd", bufs=3))
         psum_back = stack.enter_context(tc.psum_pool(name="psum_back", bufs=2))
-        psum_acc = stack.enter_context(tc.psum_pool(name="psum_acc", bufs=1))
+        psum_qk = stack.enter_context(tc.psum_pool(name="psum_qk", bufs=2))
+        psum_v = stack.enter_context(tc.psum_pool(name="psum_v", bufs=1))
 
         def load_image(b):
             image = image_pool.tile([P, PASSES, PACK, PIXELS], BF16, name="image")
@@ -82,8 +86,9 @@ def tile_transformerconvblock_pa_t_kernel(
         make_identity(nc, ident_bf16[:])
         ident_f32 = const.tile([P, P], F32)
         make_identity(nc, ident_f32[:])
-        eps = const.tile([P, 1], F32)
-        nc.vector.memset(eps[:], EPS)
+
+        minus_half = const.tile([P, 1], F32)
+        nc.vector.memset(minus_half[:], -0.5)
 
         gain_raw = const.tile([P, PASSES, PACK], BF16)
         shift_raw = const.tile([P, PASSES, PACK], BF16)
@@ -122,13 +127,13 @@ def tile_transformerconvblock_pa_t_kernel(
                 )
 
         x_t_of = {}
-        moments_of = {}
-        std_of = {}
         affine_of = {}
         z_of = {}
+        z_t_of = {}
         planes_of = {}
-        mx_of = {}
         grouped_of = {}
+        mx_of = {}
+        acc_qk_of = {}
         acc_v_of = {}
         result_of = {}
 
@@ -142,48 +147,42 @@ def tile_transformerconvblock_pa_t_kernel(
             x_t_of[n] = x_t
 
         def measure(n):
-            b, half = divmod(n, TILES_PER_IMAGE)
-            if half == 0:
-                moments_of[b] = small.tile([P, TILES_PER_IMAGE, 2], F32, name="moments")
             stats = small.tile([P, PASSES, 6], F32, name="stats")
             for c in range(PASSES):
                 nc.vector.bn_stats(out=stats[:, c, :], in_=x_t_of[n][:, c * PACK : (c + 1) * PACK, :])
-            nc.vector.bn_aggr(out=moments_of[b][:, half, :], in_=stats[:].rearrange("p c s -> p (c s)"))
-
-        def root(b):
-            std_of[b] = small.tile([P, TILES_PER_IMAGE], F32, name="std")
-            nc.scalar.activation(
-                out=std_of[b][:], in_=moments_of[b][:, :, 1], func=ACT.Sqrt, bias=eps[:, 0:1], scale=1.0
+            moments = small.tile([P, 2], F32, name="moments")
+            nc.vector.bn_aggr(out=moments[:], in_=stats[:].rearrange("p c s -> p (c s)"))
+            affine = small.tile([P, 2], F32, name="affine")
+            var_eps = small.tile([P, 1], F32, name="var_eps")
+            nc.gpsimd.tensor_scalar(out=var_eps[:], in0=moments[:, 1:2], scalar1=EPS, scalar2=None, op0=ALU.add)
+            nc.gpsimd.tensor_tensor(out=affine[:, 0:1], in0=var_eps[:], in1=minus_half[:], op=ALU.pow)
+            nc.gpsimd.tensor_scalar(
+                out=affine[:, 1:2], in0=moments[:, 0:1], scalar1=affine[:, 0:1], scalar2=-1.0,
+                op0=ALU.mult, op1=ALU.mult,
             )
-
-        def invert(b):
-            rstd = small.tile([P, TILES_PER_IMAGE], F32, name="rstd")
-            nc.vector.reciprocal(out=rstd[:], in_=std_of.pop(b)[:])
-            offset = small.tile([P, TILES_PER_IMAGE], F32, name="offset")
-            nc.vector.scalar_tensor_tensor(
-                out=offset[:], in0=moments_of.pop(b)[:, :, 0], scalar=-1.0, in1=rstd[:], op0=ALU.mult, op1=ALU.mult
-            )
-            affine_of[b] = (rstd, offset)
+            affine_of[n] = affine
 
         def centre(n):
-            b, half = divmod(n, TILES_PER_IMAGE)
-            rstd, offset = affine_of[b]
+            affine = affine_of.pop(n)
             z = z_pool.tile([P, CHANNELS], F32, name="z")
             nc.scalar.activation(
                 out=z[:], in_=x_t_of.pop(n)[:].rearrange("p g j -> p (g j)"), func=ACT.Identity,
-                bias=offset[:, half : half + 1], scale=rstd[:, half : half + 1],
+                bias=affine[:, 1:2], scale=affine[:, 0:1],
             )
             z_of[n] = z
 
-        def unflip(group, g):
-            if g == 0:
-                planes_of[group] = work.tile([P, PLANES, GROUP_PIXELS], BF16, name="planes")
+        def turn_back(group, g):
             z_t = psum_back.tile([P, GROUP_TILES, P], F32, name="z_t")
             for m in range(GROUP_TILES):
                 nc.tensor.transpose(z_t[:, m, :], z_of[group * GROUP_TILES + m][:, g * P : (g + 1) * P], ident_f32[:])
+            z_t_of[group, g] = z_t
+
+        def gain_and_shift(group, g):
+            if g == 0:
+                planes_of[group] = work.tile([P, PLANES, GROUP_PIXELS], BF16, name="planes")
             nc.scalar.activation(
-                out=planes_of[group][:, g, :], in_=z_t[:].rearrange("p m j -> p (m j)"), func=ACT.Identity,
-                bias=shift[:, g : g + 1], scale=gain[:, g : g + 1],
+                out=planes_of[group][:, g, :], in_=z_t_of.pop((group, g))[:].rearrange("p m j -> p (m j)"),
+                func=ACT.Identity, bias=shift[:, g : g + 1], scale=gain[:, g : g + 1],
             )
 
         def pack_words(group, c):
@@ -207,10 +206,13 @@ def tile_transformerconvblock_pa_t_kernel(
             b, half = divmod(n, TILES_PER_IMAGE)
             codes, scales = mx_of[n // GROUP_TILES]
             pixels = slice((n % GROUP_TILES) * P, (n % GROUP_TILES + 1) * P)
-            acc_qk = psum_acc.tile([P, QK_COLS], F32, name="acc_qk")
+            acc_qk_of[n] = psum_qk.tile([P, QK_COLS], F32, name="acc_qk")
             if half == 0:
-                acc_v_of[b] = psum_acc.tile([P, TILES_PER_IMAGE, HEAD_COLS], F32, name="acc_v")
-            for acc, cols in ((acc_qk[:], slice(0, QK_COLS)), (acc_v_of[b][:, half, :], slice(QK_COLS, OUT_COLS))):
+                acc_v_of[b] = psum_v.tile([P, TILES_PER_IMAGE, HEAD_COLS], F32, name="acc_v")
+            for acc, cols in (
+                (acc_qk_of[n][:], slice(0, QK_COLS)),
+                (acc_v_of[b][:, half, :], slice(QK_COLS, OUT_COLS)),
+            ):
                 for c in range(PASSES):
                     nc.tensor.matmul_mx(
                         out=acc,
@@ -221,48 +223,59 @@ def tile_transformerconvblock_pa_t_kernel(
                         start=(c == 0),
                         stop=(c == PASSES - 1),
                     )
-            return acc_qk
 
-        def empty(n, acc_qk):
+        def empty_v(b):
+            nc.scalar.copy(out=result_of[b][:, :, QK_COLS:OUT_COLS], in_=acc_v_of.pop(b)[:])
+
+        def empty_qk(n):
             b, half = divmod(n, TILES_PER_IMAGE)
             if half == 0:
                 result_of[b] = result_pool.tile([P, TILES_PER_IMAGE, OUT_COLS], F32, name="result")
-            result = result_of[b]
-            nc.vector.tensor_copy(out=result[:, half, 0:QK_COLS], in_=acc_qk[:])
-            if half == TILES_PER_IMAGE - 1:
-                nc.vector.tensor_copy(out=result[:, :, QK_COLS:OUT_COLS], in_=acc_v_of.pop(b)[:])
-                for o, out in enumerate(outs):
-                    nc.sync.dma_start(
-                        out=out[b * PIXELS : (b + 1) * PIXELS, :].rearrange("(m p) n -> p m n", p=P),
-                        in_=result[:, :, o * HEAD_COLS : (o + 1) * HEAD_COLS],
-                    )
+            nc.vector.tensor_copy(out=result_of[b][:, half, 0:QK_COLS], in_=acc_qk_of.pop(n)[:])
 
-        for slot in range(TILES + PROJECT_LAG):
-            measured = slot - MEASURE_LAG
-            centred = slot - CENTRE_LAG
-            unflipped = slot - UNFLIP_LAG
-            projected = slot - PROJECT_LAG
+        def store(b):
+            result = result_of.pop(b)
+            for o, out in enumerate(outs):
+                nc.sync.dma_start(
+                    out=out[b * PIXELS : (b + 1) * PIXELS, :].rearrange("(m p) n -> p m n", p=P),
+                    in_=result[:, :, o * HEAD_COLS : (o + 1) * HEAD_COLS],
+                )
 
-            if 0 <= measured - 1 < TILES and (measured - 1) % TILES_PER_IMAGE == TILES_PER_IMAGE - 1:
-                invert((measured - 1) // TILES_PER_IMAGE)
-            if 0 <= unflipped < TILES:
-                group, quarter = divmod(unflipped, GROUP_TILES)
-                for g in range(quarter * PLANES_PER_SLOT, (quarter + 1) * PLANES_PER_SLOT):
-                    unflip(group, g)
-            if 0 <= measured < TILES:
-                measure(measured)
-            if 0 <= centred < TILES:
-                centre(centred)
-            pass_done = 0 <= unflipped < TILES and (unflipped + 1) % (GROUP_TILES // PASSES) == 0
-            if pass_done:
-                pack_words(unflipped // GROUP_TILES, (unflipped % GROUP_TILES) // (GROUP_TILES // PASSES))
-            if 0 <= projected < TILES:
-                empty(projected, multiply(projected))
-            if pass_done:
-                quantise(unflipped // GROUP_TILES, (unflipped % GROUP_TILES) // (GROUP_TILES // PASSES))
+        slots_per_pass = GROUP_TILES // PASSES
+
+        def in_range(n):
+            return 0 <= n < TILES
+
+        for slot in range(TILES + EMPTY_LAG):
+            quarter = slot - QUANTISE_LAG
+            if in_range(quarter) and quarter % slots_per_pass == slots_per_pass - 1:
+                quantise(quarter // GROUP_TILES, (quarter % GROUP_TILES) // slots_per_pass)
+            quarter = slot - GAIN_LAG
+            if in_range(quarter):
+                for g in range((quarter % GROUP_TILES) * PLANES_PER_SLOT, (quarter % GROUP_TILES + 1) * PLANES_PER_SLOT):
+                    gain_and_shift(quarter // GROUP_TILES, g)
+            if in_range(slot):
+                flip(slot)
+            if in_range(slot - MEASURE_LAG):
+                measure(slot - MEASURE_LAG)
+            emptied = slot - EMPTY_LAG
+            last_of_image = in_range(emptied) and emptied % TILES_PER_IMAGE == TILES_PER_IMAGE - 1
+            if last_of_image:
+                empty_v(emptied // TILES_PER_IMAGE)
+            if in_range(slot - CENTRE_LAG):
+                centre(slot - CENTRE_LAG)
+            quarter = slot - TURN_BACK_LAG
+            if in_range(quarter):
+                for g in range((quarter % GROUP_TILES) * PLANES_PER_SLOT, (quarter % GROUP_TILES + 1) * PLANES_PER_SLOT):
+                    turn_back(quarter // GROUP_TILES, g)
+            if in_range(emptied):
+                empty_qk(emptied)
+            if last_of_image:
+                store(emptied // TILES_PER_IMAGE)
+            if in_range(slot - PROJECT_LAG):
+                multiply(slot - PROJECT_LAG)
+            quarter = slot - GAIN_LAG
+            if in_range(quarter) and quarter % slots_per_pass == slots_per_pass - 1:
+                pack_words(quarter // GROUP_TILES, (quarter % GROUP_TILES) // slots_per_pass)
             if 0 <= slot - WEIGHT_SLOT < len(weights):
                 quantise_weight(slot - WEIGHT_SLOT)
-            if slot < TILES:
-                flip(slot)
-            if 0 <= measured < TILES and measured % TILES_PER_IMAGE == TILES_PER_IMAGE - 1:
-                root(measured // TILES_PER_IMAGE)

@@ -127,6 +127,7 @@ def tile_transformerconvblock_pa_t_kernel(
                 )
 
         x_t_of = {}
+        stats_of = {}
         affine_of = {}
         z_of = {}
         z_t_of = {}
@@ -150,8 +151,11 @@ def tile_transformerconvblock_pa_t_kernel(
             stats = small.tile([P, PASSES, 6], F32, name="stats")
             for c in range(PASSES):
                 nc.vector.bn_stats(out=stats[:, c, :], in_=x_t_of[n][:, c * PACK : (c + 1) * PACK, :])
+            stats_of[n] = stats
+
+        def summarise(n):
             moments = small.tile([P, 2], F32, name="moments")
-            nc.vector.bn_aggr(out=moments[:], in_=stats[:].rearrange("p c s -> p (c s)"))
+            nc.vector.bn_aggr(out=moments[:], in_=stats_of.pop(n)[:].rearrange("p c s -> p (c s)"))
             affine = small.tile([P, 2], F32, name="affine")
             var_eps = small.tile([P, 1], F32, name="var_eps")
             nc.gpsimd.tensor_scalar(out=var_eps[:], in0=moments[:, 1:2], scalar1=EPS, scalar2=None, op0=ALU.add)
@@ -247,9 +251,6 @@ def tile_transformerconvblock_pa_t_kernel(
             return 0 <= n < TILES
 
         for slot in range(TILES + EMPTY_LAG):
-            quarter = slot - QUANTISE_LAG
-            if in_range(quarter) and quarter % slots_per_pass == slots_per_pass - 1:
-                quantise(quarter // GROUP_TILES, (quarter % GROUP_TILES) // slots_per_pass)
             quarter = slot - GAIN_LAG
             if in_range(quarter):
                 for g in range((quarter % GROUP_TILES) * PLANES_PER_SLOT, (quarter % GROUP_TILES + 1) * PLANES_PER_SLOT):
@@ -258,6 +259,9 @@ def tile_transformerconvblock_pa_t_kernel(
                 flip(slot)
             if in_range(slot - MEASURE_LAG):
                 measure(slot - MEASURE_LAG)
+            quarter = slot - QUANTISE_LAG
+            if in_range(quarter) and quarter % slots_per_pass == slots_per_pass - 1:
+                quantise(quarter // GROUP_TILES, (quarter % GROUP_TILES) // slots_per_pass)
             emptied = slot - EMPTY_LAG
             last_of_image = in_range(emptied) and emptied % TILES_PER_IMAGE == TILES_PER_IMAGE - 1
             if last_of_image:
@@ -270,6 +274,8 @@ def tile_transformerconvblock_pa_t_kernel(
                     turn_back(quarter // GROUP_TILES, g)
             if in_range(emptied):
                 empty_qk(emptied)
+            if in_range(slot - MEASURE_LAG):
+                summarise(slot - MEASURE_LAG)
             if last_of_image:
                 store(emptied // TILES_PER_IMAGE)
             if in_range(slot - PROJECT_LAG):

@@ -39,6 +39,10 @@ EMPTY_LAG = PROJECT_LAG + 1
 WEIGHT_SLOT = 4
 EARLY_IMAGES = 4
 
+SEQ = (("root", 2), ("offset", 2), ("gain", 7), ("flip", 0), ("m0", 1), ("m1", 1), ("centre", 2), ("back", 6), ("empty_qk", 13), ("aggr", 1), ("neg", 1), ("quant", 8), ("empty_v", 13), ("store", 13), ("mult", 12), ("pack", 7), ("wpack", 2), ("weight", 5),)
+V_SHARE_PERIOD = 2
+V_SHARE = 2
+
 FLOPS = 2 * IMAGES * PIXELS * CHANNELS * OUT_COLS
 
 
@@ -87,9 +91,6 @@ def tile_transformerconvblock_pa_t_kernel(
         ident_f32 = const.tile([P, P], F32)
         make_identity(nc, ident_f32[:])
 
-        minus_half = const.tile([P, 1], F32)
-        nc.vector.memset(minus_half[:], -0.5)
-
         gain_raw = const.tile([P, PASSES, PACK], BF16)
         shift_raw = const.tile([P, PASSES, PACK], BF16)
         mult_raw = const.tile([P, 1], BF16)
@@ -115,10 +116,16 @@ def tile_transformerconvblock_pa_t_kernel(
                 out=dst.rearrange("p (w i) t -> p w t i", i=4), in_=src.rearrange("p t (w i) -> p w t i", i=4)
             )
 
-        def quantise_weight(o):
+        def pack_weight(o):
             cols = slice(o * HEAD_COLS, (o + 1) * HEAD_COLS)
             for c in range(PASSES):
-                regroup(w_grouped[:, c, cols, :], w_raws[o][:, c])
+                nc.gpsimd.tensor_scalar(
+                    out=w_grouped[:, c, cols, :], in0=w_raws[o][:, c].rearrange("p t n -> p n t"),
+                    scalar1=1.0, scalar2=0.0, op0=ALU.mult, op1=ALU.add,
+                )
+
+        def quantise_weight(o):
+            cols = slice(o * HEAD_COLS, (o + 1) * HEAD_COLS)
             for c in range(PASSES):
                 nc.vector.quantize_mx(
                     out=w_codes[:, c, cols].bitcast(FP8X4),
@@ -127,6 +134,8 @@ def tile_transformerconvblock_pa_t_kernel(
                 )
 
         x_t_of = {}
+        moments_of = {}
+        neg_mean_of = {}
         stats_of = {}
         affine_of = {}
         z_of = {}
@@ -147,24 +156,29 @@ def tile_transformerconvblock_pa_t_kernel(
                     nc.tensor.transpose(x_t[:, c * PACK + t, :], image[:, c, t, pixels], ident_bf16[:])
             x_t_of[n] = x_t
 
-        def measure(n):
-            stats = small.tile([P, PASSES, 6], F32, name="stats")
-            for c in range(PASSES):
-                nc.vector.bn_stats(out=stats[:, c, :], in_=x_t_of[n][:, c * PACK : (c + 1) * PACK, :])
-            stats_of[n] = stats
+        def measure(n, c):
+            if c == 0:
+                stats_of[n] = small.tile([P, PASSES, 6], F32, name="stats")
+            nc.vector.bn_stats(out=stats_of[n][:, c, :], in_=x_t_of[n][:, c * PACK : (c + 1) * PACK, :])
 
         def summarise(n):
             moments = small.tile([P, 2], F32, name="moments")
             nc.vector.bn_aggr(out=moments[:], in_=stats_of.pop(n)[:].rearrange("p c s -> p (c s)"))
+            moments_of[n] = moments
+
+        def negate(n):
+            neg_mean = small.tile([P, 1], F32, name="neg_mean")
+            nc.vector.tensor_scalar(out=neg_mean[:], in0=moments_of[n][:, 0:1], scalar1=-1.0, scalar2=None, op0=ALU.mult)
+            neg_mean_of[n] = neg_mean
+
+        def root(n):
             affine = small.tile([P, 2], F32, name="affine")
-            var_eps = small.tile([P, 1], F32, name="var_eps")
-            nc.gpsimd.tensor_scalar(out=var_eps[:], in0=moments[:, 1:2], scalar1=EPS, scalar2=None, op0=ALU.add)
-            nc.gpsimd.tensor_tensor(out=affine[:, 0:1], in0=var_eps[:], in1=minus_half[:], op=ALU.pow)
-            nc.gpsimd.tensor_scalar(
-                out=affine[:, 1:2], in0=moments[:, 0:1], scalar1=affine[:, 0:1], scalar2=-1.0,
-                op0=ALU.mult, op1=ALU.mult,
-            )
+            nc.scalar.activation(out=affine[:, 0:1], in_=moments_of.pop(n)[:, 1:2], func=ACT.Abs_reciprocal_sqrt, bias=EPS, scale=1.0)
             affine_of[n] = affine
+
+        def offset(n):
+            affine = affine_of[n]
+            nc.scalar.activation(out=affine[:, 1:2], in_=neg_mean_of.pop(n)[:], func=ACT.Identity, bias=0.0, scale=affine[:, 0:1])
 
         def centre(n):
             affine = affine_of.pop(n)
@@ -191,7 +205,10 @@ def tile_transformerconvblock_pa_t_kernel(
 
         def pack_words(group, c):
             grouped = work.tile([P, GROUP_PIXELS, PACK], BF16, name="grouped", align_bytes=64)
-            regroup(grouped[:], planes_of[group][:, c * PACK : (c + 1) * PACK, :])
+            nc.gpsimd.tensor_scalar(
+                out=grouped[:], in0=planes_of[group][:, c * PACK : (c + 1) * PACK, :].rearrange("p t w -> p w t"),
+                scalar1=1.0, scalar2=0.0, op0=ALU.mult, op1=ALU.add,
+            )
             grouped_of[group, c] = grouped
 
         def quantise(group, c):
@@ -229,7 +246,10 @@ def tile_transformerconvblock_pa_t_kernel(
                     )
 
         def empty_v(b):
-            nc.scalar.copy(out=result_of[b][:, :, QK_COLS:OUT_COLS], in_=acc_v_of.pop(b)[:])
+            if b % V_SHARE_PERIOD < V_SHARE:
+                nc.vector.tensor_copy(out=result_of[b][:, :, QK_COLS:OUT_COLS], in_=acc_v_of.pop(b)[:])
+            else:
+                nc.scalar.copy(out=result_of[b][:, :, QK_COLS:OUT_COLS], in_=acc_v_of.pop(b)[:])
 
         def empty_qk(n):
             b, half = divmod(n, TILES_PER_IMAGE)
@@ -247,41 +267,55 @@ def tile_transformerconvblock_pa_t_kernel(
 
         slots_per_pass = GROUP_TILES // PASSES
 
-        def in_range(n):
-            return 0 <= n < TILES
+        def planes_of_quarter(q):
+            return range((q % GROUP_TILES) * PLANES_PER_SLOT, (q % GROUP_TILES + 1) * PLANES_PER_SLOT)
 
-        for slot in range(TILES + EMPTY_LAG):
-            quarter = slot - GAIN_LAG
-            if in_range(quarter):
-                for g in range((quarter % GROUP_TILES) * PLANES_PER_SLOT, (quarter % GROUP_TILES + 1) * PLANES_PER_SLOT):
-                    gain_and_shift(quarter // GROUP_TILES, g)
-            if in_range(slot):
-                flip(slot)
-            if in_range(slot - MEASURE_LAG):
-                measure(slot - MEASURE_LAG)
-            quarter = slot - QUANTISE_LAG
-            if in_range(quarter) and quarter % slots_per_pass == slots_per_pass - 1:
-                quantise(quarter // GROUP_TILES, (quarter % GROUP_TILES) // slots_per_pass)
-            emptied = slot - EMPTY_LAG
-            last_of_image = in_range(emptied) and emptied % TILES_PER_IMAGE == TILES_PER_IMAGE - 1
-            if last_of_image:
-                empty_v(emptied // TILES_PER_IMAGE)
-            if in_range(slot - CENTRE_LAG):
-                centre(slot - CENTRE_LAG)
-            quarter = slot - TURN_BACK_LAG
-            if in_range(quarter):
-                for g in range((quarter % GROUP_TILES) * PLANES_PER_SLOT, (quarter % GROUP_TILES + 1) * PLANES_PER_SLOT):
-                    turn_back(quarter // GROUP_TILES, g)
-            if in_range(emptied):
-                empty_qk(emptied)
-            if in_range(slot - MEASURE_LAG):
-                summarise(slot - MEASURE_LAG)
-            if last_of_image:
-                store(emptied // TILES_PER_IMAGE)
-            if in_range(slot - PROJECT_LAG):
-                multiply(slot - PROJECT_LAG)
-            quarter = slot - GAIN_LAG
-            if in_range(quarter) and quarter % slots_per_pass == slots_per_pass - 1:
-                pack_words(quarter // GROUP_TILES, (quarter % GROUP_TILES) // slots_per_pass)
-            if 0 <= slot - WEIGHT_SLOT < len(weights):
-                quantise_weight(slot - WEIGHT_SLOT)
+        def ends_pass(q):
+            return q % slots_per_pass == slots_per_pass - 1
+
+        def ends_image(n):
+            return n % TILES_PER_IMAGE == TILES_PER_IMAGE - 1
+
+        def st_gain(q):
+            for g in planes_of_quarter(q):
+                gain_and_shift(q // GROUP_TILES, g)
+
+        def st_back(q):
+            for g in planes_of_quarter(q):
+                turn_back(q // GROUP_TILES, g)
+
+        def st_pack(q):
+            if ends_pass(q):
+                pack_words(q // GROUP_TILES, (q % GROUP_TILES) // slots_per_pass)
+
+        def st_quant(q):
+            if ends_pass(q):
+                quantise(q // GROUP_TILES, (q % GROUP_TILES) // slots_per_pass)
+
+        def st_empty_v(n):
+            if ends_image(n):
+                empty_v(n // TILES_PER_IMAGE)
+
+        def st_store(n):
+            if ends_image(n):
+                store(n // TILES_PER_IMAGE)
+
+        def st_weight(n):
+            if n < len(weights):
+                quantise_weight(n)
+
+        def st_wpack(n):
+            if n < len(weights):
+                pack_weight(n)
+
+        stages = {
+            "flip": flip, "m0": lambda n: measure(n, 0), "m1": lambda n: measure(n, 1), "aggr": summarise, "root": root,
+            "neg": negate, "offset": offset, "centre": centre, "back": st_back, "gain": st_gain, "pack": st_pack,
+            "quant": st_quant, "mult": multiply, "empty_qk": empty_qk, "empty_v": st_empty_v, "store": st_store,
+            "weight": st_weight, "wpack": st_wpack,
+        }
+        last_lag = max(lag for name, lag in SEQ)
+        for slot in range(TILES + last_lag):
+            for name, lag in SEQ:
+                if 0 <= slot - lag < TILES:
+                    stages[name](slot - lag)

@@ -22,26 +22,23 @@ PASSES = CHANNELS // K_PASS
 PLANES = PASSES * PACK
 TILES_PER_IMAGE = PIXELS // P
 TILES = IMAGES * TILES_PER_IMAGE
-GROUP_TILES = 4
-GROUP_PIXELS = GROUP_TILES * P
-PLANES_PER_SLOT = PLANES // GROUP_TILES
 OUT_COLS = 3 * HEAD_COLS
 QK_COLS = 2 * HEAD_COLS
 EPS = 1e-5
-
-MEASURE_LAG = 1
-CENTRE_LAG = 2
-TURN_BACK_LAG = CENTRE_LAG + GROUP_TILES
-GAIN_LAG = TURN_BACK_LAG + 1
-QUANTISE_LAG = GAIN_LAG + 1
-PROJECT_LAG = QUANTISE_LAG + GROUP_TILES - 1
-EMPTY_LAG = PROJECT_LAG + 1
-WEIGHT_SLOT = 4
 EARLY_IMAGES = 4
 
-SEQ = (("root", 2), ("offset", 2), ("gain", 7), ("flip", 0), ("m0", 1), ("m1", 1), ("centre", 2), ("back", 6), ("empty_qk", 13), ("aggr", 1), ("neg", 1), ("quant", 8), ("empty_v", 13), ("store", 13), ("mult", 12), ("pack", 7), ("wpack", 2), ("weight", 5),)
-V_SHARE_PERIOD = 2
-V_SHARE = 2
+GROUP_SIZES = (4,) * 8
+MAX_GROUP = max(GROUP_SIZES)
+MEASURE_LAG = 1
+CENTRE_LAG = 2
+BACK_DELAY = 1
+GAIN_DELAY = 1
+QUANT_DELAY = 2
+MULT_DELAY = 1
+EMPTY_DELAY = 1
+SHARE_FROM = 34
+WPACK_SLOT = 2
+WQUANT_SLOT = 5
 
 FLOPS = 2 * IMAGES * PIXELS * CHANNELS * OUT_COLS
 
@@ -58,7 +55,7 @@ def tile_transformerconvblock_pa_t_kernel(
         const = stack.enter_context(tc.tile_pool(name="const", bufs=1))
         image_pool = stack.enter_context(tc.tile_pool(name="image_pool", bufs=IMAGES))
         small = stack.enter_context(tc.tile_pool(name="small", bufs=4))
-        z_pool = stack.enter_context(tc.tile_pool(name="z_pool", bufs=2 * GROUP_TILES + 2))
+        z_pool = stack.enter_context(tc.tile_pool(name="z_pool", bufs=2 * MAX_GROUP + 2))
         work = stack.enter_context(tc.tile_pool(name="work", bufs=2))
         result_pool = stack.enter_context(tc.tile_pool(name="result_pool", bufs=4))
         psum_fwd = stack.enter_context(tc.psum_pool(name="psum_fwd", bufs=3))
@@ -111,18 +108,15 @@ def tile_transformerconvblock_pa_t_kernel(
         w_codes = const.tile([P, PASSES, OUT_COLS], U32, align_bytes=64)
         w_scales = const.tile([P, PASSES, OUT_COLS], U8, align_bytes=64)
 
-        def regroup(dst, src):
-            nc.vector.tensor_copy(
-                out=dst.rearrange("p (w i) t -> p w t i", i=4), in_=src.rearrange("p t (w i) -> p w t i", i=4)
+        def interleave(dst, src):
+            nc.gpsimd.tensor_scalar(
+                out=dst, in0=src.rearrange("p t w -> p w t"), scalar1=1.0, scalar2=0.0, op0=ALU.mult, op1=ALU.add
             )
 
         def pack_weight(o):
             cols = slice(o * HEAD_COLS, (o + 1) * HEAD_COLS)
             for c in range(PASSES):
-                nc.gpsimd.tensor_scalar(
-                    out=w_grouped[:, c, cols, :], in0=w_raws[o][:, c].rearrange("p t n -> p n t"),
-                    scalar1=1.0, scalar2=0.0, op0=ALU.mult, op1=ALU.add,
-                )
+                interleave(w_grouped[:, c, cols, :], w_raws[o][:, c])
 
         def quantise_weight(o):
             cols = slice(o * HEAD_COLS, (o + 1) * HEAD_COLS)
@@ -133,10 +127,18 @@ def tile_transformerconvblock_pa_t_kernel(
                     in_=w_grouped[:, c, cols, :].rearrange("p n t -> p (n t)"),
                 )
 
+        first_of = []
+        for size in GROUP_SIZES:
+            first_of.append(sum(GROUP_SIZES[: len(first_of)]))
+        group_of = {}
+        for j, size in enumerate(GROUP_SIZES):
+            for i in range(size):
+                group_of[first_of[j] + i] = (j, i)
+
         x_t_of = {}
+        stats_of = {}
         moments_of = {}
         neg_mean_of = {}
-        stats_of = {}
         affine_of = {}
         z_of = {}
         z_t_of = {}
@@ -146,6 +148,13 @@ def tile_transformerconvblock_pa_t_kernel(
         acc_qk_of = {}
         acc_v_of = {}
         result_of = {}
+        turn = {"n": 0}
+
+        def helper(shared, usual):
+            if not shared:
+                return usual
+            turn["n"] = turn["n"] + 1
+            return "vector" if turn["n"] % 2 == 0 else "scalar"
 
         def flip(n):
             image = images[n // TILES_PER_IMAGE]
@@ -173,11 +182,12 @@ def tile_transformerconvblock_pa_t_kernel(
 
         def root(n):
             affine = small.tile([P, 2], F32, name="affine")
-            nc.scalar.activation(out=affine[:, 0:1], in_=moments_of.pop(n)[:, 1:2], func=ACT.Abs_reciprocal_sqrt, bias=EPS, scale=1.0)
+            nc.scalar.activation(out=affine[:, 0:1], in_=moments_of[n][:, 1:2], func=ACT.Abs_reciprocal_sqrt, bias=EPS, scale=1.0)
             affine_of[n] = affine
 
         def offset(n):
             affine = affine_of[n]
+            moments_of.pop(n)
             nc.scalar.activation(out=affine[:, 1:2], in_=neg_mean_of.pop(n)[:], func=ACT.Identity, bias=0.0, scale=affine[:, 0:1])
 
         def centre(n):
@@ -189,44 +199,51 @@ def tile_transformerconvblock_pa_t_kernel(
             )
             z_of[n] = z
 
-        def turn_back(group, g):
-            z_t = psum_back.tile([P, GROUP_TILES, P], F32, name="z_t")
-            for m in range(GROUP_TILES):
-                nc.tensor.transpose(z_t[:, m, :], z_of[group * GROUP_TILES + m][:, g * P : (g + 1) * P], ident_f32[:])
-            z_t_of[group, g] = z_t
+        def turn_back(j, g):
+            size = GROUP_SIZES[j]
+            z_t = psum_back.tile([P, size, P], F32, name="z_t")
+            for m in range(size):
+                nc.tensor.transpose(z_t[:, m, :], z_of[first_of[j] + m][:, g * P : (g + 1) * P], ident_f32[:])
+            z_t_of[j, g] = z_t
 
-        def gain_and_shift(group, g):
+        def gain_and_shift(j, g, shared):
+            size = GROUP_SIZES[j]
             if g == 0:
-                planes_of[group] = work.tile([P, PLANES, GROUP_PIXELS], BF16, name="planes")
-            nc.scalar.activation(
-                out=planes_of[group][:, g, :], in_=z_t_of.pop((group, g))[:].rearrange("p m j -> p (m j)"),
-                func=ACT.Identity, bias=shift[:, g : g + 1], scale=gain[:, g : g + 1],
-            )
+                planes_of[j] = work.tile([P, PLANES, size * P], BF16, name="planes")
+            z_t = z_t_of.pop((j, g))[:].rearrange("p m j -> p (m j)")
+            if helper(shared, "scalar") == "vector":
+                nc.vector.tensor_scalar(
+                    out=planes_of[j][:, g, :], in0=z_t, scalar1=gain[:, g : g + 1], scalar2=shift[:, g : g + 1],
+                    op0=ALU.mult, op1=ALU.add,
+                )
+            else:
+                nc.scalar.activation(
+                    out=planes_of[j][:, g, :], in_=z_t, func=ACT.Identity, bias=shift[:, g : g + 1], scale=gain[:, g : g + 1],
+                )
 
-        def pack_words(group, c):
-            grouped = work.tile([P, GROUP_PIXELS, PACK], BF16, name="grouped", align_bytes=64)
-            nc.gpsimd.tensor_scalar(
-                out=grouped[:], in0=planes_of[group][:, c * PACK : (c + 1) * PACK, :].rearrange("p t w -> p w t"),
-                scalar1=1.0, scalar2=0.0, op0=ALU.mult, op1=ALU.add,
-            )
-            grouped_of[group, c] = grouped
+        def pack_words(j, c):
+            grouped = work.tile([P, GROUP_SIZES[j] * P, PACK], BF16, name="grouped", align_bytes=64)
+            interleave(grouped[:], planes_of[j][:, c * PACK : (c + 1) * PACK, :])
+            grouped_of[j, c] = grouped
 
-        def quantise(group, c):
+        def quantise(j, c):
+            size = GROUP_SIZES[j]
             if c == 0:
-                codes = work.tile([P, PASSES, GROUP_PIXELS], U32, name="codes", align_bytes=64)
-                scales = work.tile([P, PASSES, GROUP_PIXELS], U8, name="scales", align_bytes=64)
-                mx_of[group] = (codes, scales)
-            codes, scales = mx_of[group]
+                codes = work.tile([P, PASSES, size * P], U32, name="codes", align_bytes=64)
+                scales = work.tile([P, PASSES, size * P], U8, name="scales", align_bytes=64)
+                mx_of[j] = (codes, scales)
+            codes, scales = mx_of[j]
             nc.vector.quantize_mx(
                 out=codes[:, c, :].bitcast(FP8X4),
                 scales=scales[:, c, :],
-                in_=grouped_of.pop((group, c))[:].rearrange("p w t -> p (w t)"),
+                in_=grouped_of.pop((j, c))[:].rearrange("p w t -> p (w t)"),
             )
 
         def multiply(n):
             b, half = divmod(n, TILES_PER_IMAGE)
-            codes, scales = mx_of[n // GROUP_TILES]
-            pixels = slice((n % GROUP_TILES) * P, (n % GROUP_TILES + 1) * P)
+            j, i = group_of[n]
+            codes, scales = mx_of[j]
+            pixels = slice(i * P, (i + 1) * P)
             acc_qk_of[n] = psum_qk.tile([P, QK_COLS], F32, name="acc_qk")
             if half == 0:
                 acc_v_of[b] = psum_v.tile([P, TILES_PER_IMAGE, HEAD_COLS], F32, name="acc_v")
@@ -245,17 +262,20 @@ def tile_transformerconvblock_pa_t_kernel(
                         stop=(c == PASSES - 1),
                     )
 
-        def empty_v(b):
-            if b % V_SHARE_PERIOD < V_SHARE:
-                nc.vector.tensor_copy(out=result_of[b][:, :, QK_COLS:OUT_COLS], in_=acc_v_of.pop(b)[:])
+        def copy_out(dst, src, shared):
+            if helper(shared, "vector") == "vector":
+                nc.vector.tensor_copy(out=dst, in_=src)
             else:
-                nc.scalar.copy(out=result_of[b][:, :, QK_COLS:OUT_COLS], in_=acc_v_of.pop(b)[:])
+                nc.scalar.copy(out=dst, in_=src)
 
-        def empty_qk(n):
+        def empty_qk(n, shared):
             b, half = divmod(n, TILES_PER_IMAGE)
             if half == 0:
                 result_of[b] = result_pool.tile([P, TILES_PER_IMAGE, OUT_COLS], F32, name="result")
-            nc.vector.tensor_copy(out=result_of[b][:, half, 0:QK_COLS], in_=acc_qk_of.pop(n)[:])
+            copy_out(result_of[b][:, half, 0:QK_COLS], acc_qk_of.pop(n)[:], shared)
+
+        def empty_v(b, shared):
+            copy_out(result_of[b][:, :, QK_COLS:OUT_COLS], acc_v_of.pop(b)[:], shared)
 
         def store(b):
             result = result_of.pop(b)
@@ -265,57 +285,69 @@ def tile_transformerconvblock_pa_t_kernel(
                     in_=result[:, :, o * HEAD_COLS : (o + 1) * HEAD_COLS],
                 )
 
-        slots_per_pass = GROUP_TILES // PASSES
+        backs = {}
+        gains = {}
+        packs = {}
+        quants = {}
+        mults = {}
+        empties = {}
+        next_mult = 0
+        for j, size in enumerate(GROUP_SIZES):
+            ready = first_of[j] + size - 1 + CENTRE_LAG
+            for g in range(PLANES):
+                s = ready + BACK_DELAY + (g * size) // PLANES
+                backs.setdefault(s, []).append((j, g))
+                gains.setdefault(s + GAIN_DELAY, []).append((j, g))
+                if g % PACK == PACK - 1:
+                    packs.setdefault(s + GAIN_DELAY, []).append((j, g // PACK))
+                    quants.setdefault(s + GAIN_DELAY + QUANT_DELAY, []).append((j, g // PACK))
+            s = max(s + GAIN_DELAY + QUANT_DELAY + MULT_DELAY, next_mult)
+            for i in range(size):
+                mults.setdefault(s + i, []).append(first_of[j] + i)
+                empties.setdefault(s + i + EMPTY_DELAY, []).append(first_of[j] + i)
+            next_mult = s + size
 
-        def planes_of_quarter(q):
-            return range((q % GROUP_TILES) * PLANES_PER_SLOT, (q % GROUP_TILES + 1) * PLANES_PER_SLOT)
+        def in_range(n):
+            return 0 <= n < TILES
 
-        def ends_pass(q):
-            return q % slots_per_pass == slots_per_pass - 1
-
-        def ends_image(n):
-            return n % TILES_PER_IMAGE == TILES_PER_IMAGE - 1
-
-        def st_gain(q):
-            for g in planes_of_quarter(q):
-                gain_and_shift(q // GROUP_TILES, g)
-
-        def st_back(q):
-            for g in planes_of_quarter(q):
-                turn_back(q // GROUP_TILES, g)
-
-        def st_pack(q):
-            if ends_pass(q):
-                pack_words(q // GROUP_TILES, (q % GROUP_TILES) // slots_per_pass)
-
-        def st_quant(q):
-            if ends_pass(q):
-                quantise(q // GROUP_TILES, (q % GROUP_TILES) // slots_per_pass)
-
-        def st_empty_v(n):
-            if ends_image(n):
-                empty_v(n // TILES_PER_IMAGE)
-
-        def st_store(n):
-            if ends_image(n):
-                store(n // TILES_PER_IMAGE)
-
-        def st_weight(n):
-            if n < len(weights):
-                quantise_weight(n)
-
-        def st_wpack(n):
-            if n < len(weights):
-                pack_weight(n)
-
-        stages = {
-            "flip": flip, "m0": lambda n: measure(n, 0), "m1": lambda n: measure(n, 1), "aggr": summarise, "root": root,
-            "neg": negate, "offset": offset, "centre": centre, "back": st_back, "gain": st_gain, "pack": st_pack,
-            "quant": st_quant, "mult": multiply, "empty_qk": empty_qk, "empty_v": st_empty_v, "store": st_store,
-            "weight": st_weight, "wpack": st_wpack,
-        }
-        last_lag = max(lag for name, lag in SEQ)
-        for slot in range(TILES + last_lag):
-            for name, lag in SEQ:
-                if 0 <= slot - lag < TILES:
-                    stages[name](slot - lag)
+        for slot in range(max(empties) + 1):
+            shared = slot >= SHARE_FROM
+            slot_gains = gains.get(slot, [])
+            if in_range(slot - CENTRE_LAG):
+                root(slot - CENTRE_LAG)
+            for j, g in slot_gains[: (len(slot_gains) + 1) // 2]:
+                gain_and_shift(j, g, shared)
+            if in_range(slot):
+                flip(slot)
+            if in_range(slot - MEASURE_LAG):
+                measure(slot - MEASURE_LAG, 0)
+            if in_range(slot - CENTRE_LAG):
+                negate(slot - CENTRE_LAG)
+            if in_range(slot - MEASURE_LAG):
+                measure(slot - MEASURE_LAG, 1)
+            if in_range(slot - CENTRE_LAG):
+                offset(slot - CENTRE_LAG)
+            for j, g in slot_gains[(len(slot_gains) + 1) // 2 :]:
+                gain_and_shift(j, g, shared)
+            if in_range(slot - CENTRE_LAG):
+                centre(slot - CENTRE_LAG)
+            for j, g in backs.get(slot, []):
+                turn_back(j, g)
+            for n in empties.get(slot, []):
+                empty_qk(n, shared)
+            if in_range(slot - MEASURE_LAG):
+                summarise(slot - MEASURE_LAG)
+            for j, c in quants.get(slot, []):
+                quantise(j, c)
+            for n in empties.get(slot, []):
+                if n % TILES_PER_IMAGE == TILES_PER_IMAGE - 1:
+                    empty_v(n // TILES_PER_IMAGE, shared)
+                    store(n // TILES_PER_IMAGE)
+            for n in mults.get(slot, []):
+                multiply(n)
+            for j, c in packs.get(slot, []):
+                pack_words(j, c)
+            if 0 <= slot - WPACK_SLOT < len(weights):
+                pack_weight(slot - WPACK_SLOT)
+            if 0 <= slot - WQUANT_SLOT < len(weights):
+                quantise_weight(slot - WQUANT_SLOT)

@@ -37,6 +37,10 @@ QUANT_DELAY = 2
 MULT_DELAY = 1
 EMPTY_DELAY = 1
 SHARE_FROM = 34
+DRAIN_SPEED = 1
+DRAIN_BANKS = 0
+LAST_PACK_V = 0
+PACK_PIXELS = 128
 WPACK_SLOT = 2
 WQUANT_SLOT = 5
 
@@ -201,7 +205,10 @@ def tile_transformerconvblock_pa_t_kernel(
 
         def turn_back(j, g):
             size = GROUP_SIZES[j]
-            z_t = psum_back.tile([P, size, P], F32, name="z_t")
+            if DRAIN_BANKS and j == len(GROUP_SIZES) - 1 and g % 2 == 1:
+                z_t = psum_fwd.tile([P, size, P], F32, name="x_t")
+            else:
+                z_t = psum_back.tile([P, size, P], F32, name="z_t")
             for m in range(size):
                 nc.tensor.transpose(z_t[:, m, :], z_of[first_of[j] + m][:, g * P : (g + 1) * P], ident_f32[:])
             z_t_of[j, g] = z_t
@@ -223,7 +230,14 @@ def tile_transformerconvblock_pa_t_kernel(
 
         def pack_words(j, c):
             grouped = work.tile([P, GROUP_SIZES[j] * P, PACK], BF16, name="grouped", align_bytes=64)
-            interleave(grouped[:], planes_of[j][:, c * PACK : (c + 1) * PACK, :])
+            if LAST_PACK_V and j == len(GROUP_SIZES) - 1 and c == PASSES - 1:
+                nc.vector.tensor_copy(
+                    out=grouped[:].rearrange("p (w i) t -> p w t i", i=4),
+                    in_=planes_of[j][:, c * PACK : (c + 1) * PACK, :].rearrange("p t (w i) -> p w t i", i=4),
+                )
+            else:
+                for m in range(0, GROUP_SIZES[j] * P, PACK_PIXELS):
+                    interleave(grouped[:, m : m + PACK_PIXELS, :], planes_of[j][:, c * PACK : (c + 1) * PACK, m : m + PACK_PIXELS])
             grouped_of[j, c] = grouped
 
         def quantise(j, c):
@@ -295,7 +309,7 @@ def tile_transformerconvblock_pa_t_kernel(
         for j, size in enumerate(GROUP_SIZES):
             ready = first_of[j] + size - 1 + CENTRE_LAG
             for g in range(PLANES):
-                s = ready + BACK_DELAY + (g * size) // PLANES
+                s = ready + BACK_DELAY + (g * size) // (PLANES * (DRAIN_SPEED if ready + BACK_DELAY >= SHARE_FROM else 1))
                 backs.setdefault(s, []).append((j, g))
                 gains.setdefault(s + GAIN_DELAY, []).append((j, g))
                 if g % PACK == PACK - 1:

@@ -41,6 +41,8 @@ DRAIN_SPEED = 1
 DRAIN_BANKS = 0
 LAST_PACK_V = 0
 PACK_PIXELS = 128
+MULT_POS = 2
+GAIN_SLOT = 4
 WPACK_SLOT = 2
 WQUANT_SLOT = 5
 
@@ -83,30 +85,36 @@ def tile_transformerconvblock_pa_t_kernel(
             )
             return w_raw
 
+        gain_raw = const.tile([P, PASSES, PACK], BF16)
+        shift_raw = const.tile([P, PASSES, PACK], BF16)
+        mult_raw = const.tile([P, 1], BF16)
         images = [load_image(b) for b in range(EARLY_IMAGES)]
+        nc.sync.dma_start(out=gain_raw[:], in_=ln1_w.rearrange("(c p t) -> p c t", c=PASSES, p=P))
+        nc.sync.dma_start(out=shift_raw[:], in_=ln1_b.rearrange("(c p t) -> p c t", c=PASSES, p=P))
+        nc.sync.dma_start(out=mult_raw[:], in_=scale_norm1.partition_broadcast(P))
         w_raws = [load_weight(o) for o in range(len(weights))]
         images.extend([load_image(b) for b in range(EARLY_IMAGES, IMAGES)])
+
+        warm = const.tile([P, 1], F32)
+        nc.vector.memset(warm[:], 1.0)
+        nc.scalar.activation(out=warm[:], in_=warm[:], func=ACT.Abs_reciprocal_sqrt, bias=0.0, scale=1.0)
 
         ident_bf16 = const.tile([P, P], BF16)
         make_identity(nc, ident_bf16[:])
         ident_f32 = const.tile([P, P], F32)
         make_identity(nc, ident_f32[:])
 
-        gain_raw = const.tile([P, PASSES, PACK], BF16)
-        shift_raw = const.tile([P, PASSES, PACK], BF16)
-        mult_raw = const.tile([P, 1], BF16)
-        nc.scalar.dma_start(out=gain_raw[:], in_=ln1_w.rearrange("(c p t) -> p c t", c=PASSES, p=P))
-        nc.scalar.dma_start(out=shift_raw[:], in_=ln1_b.rearrange("(c p t) -> p c t", c=PASSES, p=P))
-        nc.scalar.dma_start(out=mult_raw[:], in_=scale_norm1.partition_broadcast(P))
         mult = const.tile([P, 1], F32)
-        nc.vector.tensor_copy(out=mult[:], in_=mult_raw[:])
         gain = const.tile([P, PLANES], F32)
         shift = const.tile([P, PLANES], F32)
-        for scaled, raw in ((gain, gain_raw), (shift, shift_raw)):
-            nc.vector.tensor_scalar(
-                out=scaled[:], in0=raw[:].rearrange("p c t -> p (c t)"),
-                scalar1=mult[:, 0:1], scalar2=None, op0=ALU.mult,
-            )
+
+        def scale_gain_and_shift():
+            nc.vector.tensor_copy(out=mult[:], in_=mult_raw[:])
+            for scaled, raw in ((gain, gain_raw), (shift, shift_raw)):
+                nc.vector.tensor_scalar(
+                    out=scaled[:], in0=raw[:].rearrange("p c t -> p (c t)"),
+                    scalar1=mult[:, 0:1], scalar2=None, op0=ALU.mult,
+                )
 
         w_grouped = const.tile([P, PASSES, OUT_COLS, PACK], BF16, align_bytes=64)
         w_codes = const.tile([P, PASSES, OUT_COLS], U32, align_bytes=64)
@@ -331,8 +339,14 @@ def tile_transformerconvblock_pa_t_kernel(
                 root(slot - CENTRE_LAG)
             for j, g in slot_gains[: (len(slot_gains) + 1) // 2]:
                 gain_and_shift(j, g, shared)
+            if MULT_POS == 0:
+                for n in mults.get(slot, []):
+                    multiply(n)
             if in_range(slot):
                 flip(slot)
+            if MULT_POS == 1:
+                for n in mults.get(slot, []):
+                    multiply(n)
             if in_range(slot - MEASURE_LAG):
                 measure(slot - MEASURE_LAG, 0)
             if in_range(slot - CENTRE_LAG):
@@ -357,10 +371,13 @@ def tile_transformerconvblock_pa_t_kernel(
                 if n % TILES_PER_IMAGE == TILES_PER_IMAGE - 1:
                     empty_v(n // TILES_PER_IMAGE, shared)
                     store(n // TILES_PER_IMAGE)
-            for n in mults.get(slot, []):
-                multiply(n)
+            if MULT_POS == 2:
+                for n in mults.get(slot, []):
+                    multiply(n)
             for j, c in packs.get(slot, []):
                 pack_words(j, c)
+            if slot == GAIN_SLOT:
+                scale_gain_and_shift()
             if 0 <= slot - WPACK_SLOT < len(weights):
                 pack_weight(slot - WPACK_SLOT)
             if 0 <= slot - WQUANT_SLOT < len(weights):

@@ -27,14 +27,14 @@ QK_COLS = 2 * HEAD_COLS
 EPS = 1e-5
 EARLY_IMAGES = 4
 
-GROUP_SIZES = (4,) * 8
+GROUP_SIZES = (2,) * 16
 MAX_GROUP = max(GROUP_SIZES)
 MEASURE_LAG = 1
 CENTRE_LAG = 2
 BACK_DELAY = 1
 GAIN_DELAY = 1
 QUANT_DELAY = 2
-MULT_DELAY = 1
+MULT_DELAY = 0
 EMPTY_DELAY = 1
 SHARE_FROM = 34
 DRAIN_SPEED = 1
@@ -42,6 +42,7 @@ DRAIN_BANKS = 0
 LAST_PACK_V = 0
 PACK_PIXELS = 128
 MULT_POS = 2
+BANK_TILES = 4
 GAIN_SLOT = 4
 WPACK_SLOT = 2
 WQUANT_SLOT = 5
@@ -154,6 +155,7 @@ def tile_transformerconvblock_pa_t_kernel(
         affine_of = {}
         z_of = {}
         z_t_of = {}
+        bank_of = {}
         planes_of = {}
         grouped_of = {}
         mx_of = {}
@@ -213,10 +215,10 @@ def tile_transformerconvblock_pa_t_kernel(
 
         def turn_back(j, g):
             size = GROUP_SIZES[j]
-            if DRAIN_BANKS and j == len(GROUP_SIZES) - 1 and g % 2 == 1:
-                z_t = psum_fwd.tile([P, size, P], F32, name="x_t")
-            else:
-                z_t = psum_back.tile([P, size, P], F32, name="z_t")
+            per_bank = BANK_TILES // size
+            if g % per_bank == 0:
+                bank_of[j] = psum_back.tile([P, per_bank, size, P], F32, name="z_t")
+            z_t = bank_of[j][:, g % per_bank]
             for m in range(size):
                 nc.tensor.transpose(z_t[:, m, :], z_of[first_of[j] + m][:, g * P : (g + 1) * P], ident_f32[:])
             z_t_of[j, g] = z_t
@@ -225,7 +227,7 @@ def tile_transformerconvblock_pa_t_kernel(
             size = GROUP_SIZES[j]
             if g == 0:
                 planes_of[j] = work.tile([P, PLANES, size * P], BF16, name="planes")
-            z_t = z_t_of.pop((j, g))[:].rearrange("p m j -> p (m j)")
+            z_t = z_t_of.pop((j, g)).rearrange("p m j -> p (m j)")
             if helper(shared, "scalar") == "vector":
                 nc.vector.tensor_scalar(
                     out=planes_of[j][:, g, :], in0=z_t, scalar1=gain[:, g : g + 1], scalar2=shift[:, g : g + 1],

@@ -39,10 +39,16 @@ EMPTY_DELAY = 1
 SHARE_FROM = 34
 DRAIN_SPEED = 1
 DRAIN_BANKS = 0
-LAST_PACK_V = 0
+LAST_PACK_V = 1
 PACK_PIXELS = 128
 MULT_POS = 2
 BANK_TILES = 4
+LAST_FAST = 1
+DRAIN_COPY = 0
+COPY_SHARE_FROM = 34
+VECTOR_PLANES = ()
+SPLIT_IMAGES = 1
+FAST_QUANTS = 2
 GAIN_SLOT = 4
 WPACK_SLOT = 2
 WQUANT_SLOT = 5
@@ -63,7 +69,7 @@ def tile_transformerconvblock_pa_t_kernel(
         image_pool = stack.enter_context(tc.tile_pool(name="image_pool", bufs=IMAGES))
         small = stack.enter_context(tc.tile_pool(name="small", bufs=4))
         z_pool = stack.enter_context(tc.tile_pool(name="z_pool", bufs=2 * MAX_GROUP + 2))
-        work = stack.enter_context(tc.tile_pool(name="work", bufs=2))
+        work = stack.enter_context(tc.tile_pool(name="work", bufs=3))
         result_pool = stack.enter_context(tc.tile_pool(name="result_pool", bufs=4))
         psum_fwd = stack.enter_context(tc.psum_pool(name="psum_fwd", bufs=3))
         psum_back = stack.enter_context(tc.psum_pool(name="psum_back", bufs=2))
@@ -72,10 +78,12 @@ def tile_transformerconvblock_pa_t_kernel(
 
         def load_image(b):
             image = image_pool.tile([P, PASSES, PACK, PIXELS], BF16, name="image")
-            nc.sync.dma_start(
-                out=image[:].rearrange("p c t w -> p c (t w)"),
-                in_=x[b].rearrange("(c p t) h w -> p c (t h w)", c=PASSES, p=P),
-            )
+            source = x[b].rearrange("(c p t) h w -> p c (t h w)", c=PASSES, p=P)
+            if b < SPLIT_IMAGES:
+                for c in range(PASSES):
+                    nc.sync.dma_start(out=image[:, c].rearrange("p t w -> p (t w)"), in_=source[:, c])
+            else:
+                nc.sync.dma_start(out=image[:].rearrange("p c t w -> p c (t w)"), in_=source)
             return image
 
         def load_weight(o):
@@ -217,7 +225,10 @@ def tile_transformerconvblock_pa_t_kernel(
             size = GROUP_SIZES[j]
             per_bank = BANK_TILES // size
             if g % per_bank == 0:
-                bank_of[j] = psum_back.tile([P, per_bank, size, P], F32, name="z_t")
+                if LAST_FAST and j == len(GROUP_SIZES) - 1 and (g // per_bank) % 2 == 1:
+                    bank_of[j] = psum_fwd.tile([P, per_bank, size, P], F32, name="x_t")
+                else:
+                    bank_of[j] = psum_back.tile([P, per_bank, size, P], F32, name="z_t")
             z_t = bank_of[j][:, g % per_bank]
             for m in range(size):
                 nc.tensor.transpose(z_t[:, m, :], z_of[first_of[j] + m][:, g * P : (g + 1) * P], ident_f32[:])
@@ -228,7 +239,7 @@ def tile_transformerconvblock_pa_t_kernel(
             if g == 0:
                 planes_of[j] = work.tile([P, PLANES, size * P], BF16, name="planes")
             z_t = z_t_of.pop((j, g)).rearrange("p m j -> p (m j)")
-            if helper(shared, "scalar") == "vector":
+            if g in VECTOR_PLANES or (shared and (g // (BANK_TILES // size)) % 2 == 1):
                 nc.vector.tensor_scalar(
                     out=planes_of[j][:, g, :], in0=z_t, scalar1=gain[:, g : g + 1], scalar2=shift[:, g : g + 1],
                     op0=ALU.mult, op1=ALU.add,
@@ -240,7 +251,7 @@ def tile_transformerconvblock_pa_t_kernel(
 
         def pack_words(j, c):
             grouped = work.tile([P, GROUP_SIZES[j] * P, PACK], BF16, name="grouped", align_bytes=64)
-            if LAST_PACK_V and j == len(GROUP_SIZES) - 1 and c == PASSES - 1:
+            if j >= len(GROUP_SIZES) - LAST_PACK_V:
                 nc.vector.tensor_copy(
                     out=grouped[:].rearrange("p (w i) t -> p w t i", i=4),
                     in_=planes_of[j][:, c * PACK : (c + 1) * PACK, :].rearrange("p t (w i) -> p w t i", i=4),
@@ -287,7 +298,7 @@ def tile_transformerconvblock_pa_t_kernel(
                     )
 
         def copy_out(dst, src, shared):
-            if helper(shared, "vector") == "vector":
+            if (DRAIN_COPY == 0 and helper(shared, "vector") == "vector") or (DRAIN_COPY == 1 and not shared):
                 nc.vector.tensor_copy(out=dst, in_=src)
             else:
                 nc.scalar.copy(out=dst, in_=src)
@@ -319,13 +330,15 @@ def tile_transformerconvblock_pa_t_kernel(
         for j, size in enumerate(GROUP_SIZES):
             ready = first_of[j] + size - 1 + CENTRE_LAG
             for g in range(PLANES):
-                s = ready + BACK_DELAY + (g * size) // (PLANES * (DRAIN_SPEED if ready + BACK_DELAY >= SHARE_FROM else 1))
+                fast = LAST_FAST and j == len(GROUP_SIZES) - 1
+                s = ready + BACK_DELAY + (0 if fast else (g * size) // PLANES)
+                quant_delay = 1 if j >= len(GROUP_SIZES) - FAST_QUANTS else QUANT_DELAY
                 backs.setdefault(s, []).append((j, g))
                 gains.setdefault(s + GAIN_DELAY, []).append((j, g))
                 if g % PACK == PACK - 1:
                     packs.setdefault(s + GAIN_DELAY, []).append((j, g // PACK))
-                    quants.setdefault(s + GAIN_DELAY + QUANT_DELAY, []).append((j, g // PACK))
-            s = max(s + GAIN_DELAY + QUANT_DELAY + MULT_DELAY, next_mult)
+                    quants.setdefault(s + GAIN_DELAY + quant_delay, []).append((j, g // PACK))
+            s = max(s + GAIN_DELAY + quant_delay + MULT_DELAY, next_mult)
             for i in range(size):
                 mults.setdefault(s + i, []).append(first_of[j] + i)
                 empties.setdefault(s + i + EMPTY_DELAY, []).append(first_of[j] + i)
@@ -364,14 +377,14 @@ def tile_transformerconvblock_pa_t_kernel(
             for j, g in backs.get(slot, []):
                 turn_back(j, g)
             for n in empties.get(slot, []):
-                empty_qk(n, shared)
+                empty_qk(n, slot >= COPY_SHARE_FROM)
             if in_range(slot - MEASURE_LAG):
                 summarise(slot - MEASURE_LAG)
             for j, c in quants.get(slot, []):
                 quantise(j, c)
             for n in empties.get(slot, []):
                 if n % TILES_PER_IMAGE == TILES_PER_IMAGE - 1:
-                    empty_v(n // TILES_PER_IMAGE, shared)
+                    empty_v(n // TILES_PER_IMAGE, slot >= COPY_SHARE_FROM)
                     store(n // TILES_PER_IMAGE)
             if MULT_POS == 2:
                 for n in mults.get(slot, []):

@@ -199,7 +199,7 @@ def tile_transformerconvblock_pa_t_kernel(
 
         def negate(n):
             neg_mean = small.tile([P, 1], F32, name="neg_mean")
-            nc.vector.tensor_scalar(out=neg_mean[:], in0=moments_of[n][:, 0:1], scalar1=-1.0, scalar2=None, op0=ALU.mult)
+            nc.vector.tensor_reduce(out=neg_mean[:], in_=moments_of[n][:, 0:1], axis=mybir.AxisListType.X, op=ALU.add, negate=True)
             neg_mean_of[n] = neg_mean
 
         def root(n):

@@ -159,7 +159,7 @@ def tile_transformerconvblock_pa_t_kernel(
         x_t_of = {}
         stats_of = {}
         moments_of = {}
-        neg_mean_of = {}
+        neg_ratio_of = {}
         affine_of = {}
         z_of = {}
         z_t_of = {}
@@ -197,27 +197,24 @@ def tile_transformerconvblock_pa_t_kernel(
             nc.vector.bn_aggr(out=moments[:], in_=stats_of.pop(n)[:].rearrange("p c s -> p (c s)"))
             moments_of[n] = moments
 
-        def negate(n):
-            neg_mean = small.tile([P, 1], F32, name="neg_mean")
-            nc.vector.tensor_reduce(out=neg_mean[:], in_=moments_of[n][:, 0:1], axis=mybir.AxisListType.X, op=ALU.add, negate=True)
-            neg_mean_of[n] = neg_mean
-
         def root(n):
-            affine = small.tile([P, 2], F32, name="affine")
+            affine = small.tile([P, 1], F32, name="affine")
             nc.scalar.activation(out=affine[:, 0:1], in_=moments_of[n][:, 1:2], func=ACT.Abs_reciprocal_sqrt, bias=EPS, scale=1.0)
             affine_of[n] = affine
 
         def offset(n):
-            affine = affine_of[n]
-            moments_of.pop(n)
-            nc.scalar.activation(out=affine[:, 1:2], in_=neg_mean_of.pop(n)[:], func=ACT.Identity, bias=0.0, scale=affine[:, 0:1])
+            neg_ratio = small.tile([P, 1], F32, name="neg_ratio")
+            nc.vector.scalar_tensor_tensor(
+                out=neg_ratio[:], in0=moments_of.pop(n)[:, 0:1], scalar=-1.0, in1=affine_of[n][:, 0:1], op0=ALU.mult, op1=ALU.mult
+            )
+            neg_ratio_of[n] = neg_ratio
 
         def centre(n):
             affine = affine_of.pop(n)
             z = z_pool.tile([P, CHANNELS], F32, name="z")
             nc.scalar.activation(
                 out=z[:], in_=x_t_of.pop(n)[:].rearrange("p g j -> p (g j)"), func=ACT.Identity,
-                bias=affine[:, 1:2], scale=affine[:, 0:1],
+                bias=neg_ratio_of.pop(n)[:, 0:1], scale=affine[:, 0:1],
             )
             z_of[n] = z
 
@@ -365,11 +362,9 @@ def tile_transformerconvblock_pa_t_kernel(
             if in_range(slot - MEASURE_LAG):
                 measure(slot - MEASURE_LAG, 0)
             if in_range(slot - CENTRE_LAG):
-                negate(slot - CENTRE_LAG)
+                offset(slot - CENTRE_LAG)
             if in_range(slot - MEASURE_LAG):
                 measure(slot - MEASURE_LAG, 1)
-            if in_range(slot - CENTRE_LAG):
-                offset(slot - CENTRE_LAG)
             for j, g in slot_gains[(len(slot_gains) + 1) // 2 :]:
                 gain_and_shift(j, g, shared)
             if in_range(slot - CENTRE_LAG):

@@ -204,8 +204,8 @@ def tile_transformerconvblock_pa_t_kernel(
 
         def offset(n):
             neg_ratio = small.tile([P, 1], F32, name="neg_ratio")
-            nc.vector.scalar_tensor_tensor(
-                out=neg_ratio[:], in0=moments_of.pop(n)[:, 0:1], scalar=-1.0, in1=affine_of[n][:, 0:1], op0=ALU.mult, op1=ALU.mult
+            nc.vector.tensor_scalar(
+                out=neg_ratio[:], in0=moments_of.pop(n)[:, 0:1], scalar1=affine_of[n][:, 0:1], scalar2=-1.0, op0=ALU.mult, op1=ALU.mult
             )
             neg_ratio_of[n] = neg_ratio
 

@@ -70,6 +70,7 @@ def tile_transformerconvblock_pa_t_kernel(
         small = stack.enter_context(tc.tile_pool(name="small", bufs=4))
         z_pool = stack.enter_context(tc.tile_pool(name="z_pool", bufs=2 * MAX_GROUP + 2))
         work = stack.enter_context(tc.tile_pool(name="work", bufs=3))
+        grouped_pool = stack.enter_context(tc.tile_pool(name="grouped_pool", bufs=2))
         result_pool = stack.enter_context(tc.tile_pool(name="result_pool", bufs=4))
         psum_fwd = stack.enter_context(tc.psum_pool(name="psum_fwd", bufs=3))
         psum_back = stack.enter_context(tc.psum_pool(name="psum_back", bufs=2))
@@ -247,7 +248,7 @@ def tile_transformerconvblock_pa_t_kernel(
                 )
 
         def pack_words(j, c):
-            grouped = work.tile([P, GROUP_SIZES[j] * P, PACK], BF16, name="grouped", align_bytes=64)
+            grouped = grouped_pool.tile([P, GROUP_SIZES[j] * P, PACK], BF16, name="grouped", align_bytes=64)
             if j >= len(GROUP_SIZES) - LAST_PACK_V:
                 nc.vector.tensor_copy(
                     out=grouped[:].rearrange("p (w i) t -> p w t i", i=4),

@@ -40,7 +40,7 @@ SHARE_FROM = 34
 DRAIN_SPEED = 1
 DRAIN_BANKS = 0
 LAST_PACK_V = 1
-PACK_PIXELS = 128
+PACK_PIXELS = 256
 MULT_POS = 2
 BANK_TILES = 4
 LAST_FAST = 1

@@ -72,10 +72,9 @@ def tile_transformerconvblock_pa_t_kernel(
         work = stack.enter_context(tc.tile_pool(name="work", bufs=3))
         grouped_pool = stack.enter_context(tc.tile_pool(name="grouped_pool", bufs=2))
         result_pool = stack.enter_context(tc.tile_pool(name="result_pool", bufs=4))
-        psum_fwd = stack.enter_context(tc.psum_pool(name="psum_fwd", bufs=3))
+        psum_fwd = stack.enter_context(tc.psum_pool(name="psum_fwd", bufs=4))
         psum_back = stack.enter_context(tc.psum_pool(name="psum_back", bufs=2))
-        psum_qk = stack.enter_context(tc.psum_pool(name="psum_qk", bufs=2))
-        psum_v = stack.enter_context(tc.psum_pool(name="psum_v", bufs=1))
+        psum_acc = stack.enter_context(tc.psum_pool(name="psum_acc", bufs=2))
 
         def load_image(b):
             image = image_pool.tile([P, PASSES, PACK, PIXELS], BF16, name="image")
@@ -109,8 +108,6 @@ def tile_transformerconvblock_pa_t_kernel(
         nc.vector.memset(warm[:], 1.0)
         nc.scalar.activation(out=warm[:], in_=warm[:], func=ACT.Abs_reciprocal_sqrt, bias=0.0, scale=1.0)
 
-        ident_bf16 = const.tile([P, P], BF16)
-        make_identity(nc, ident_bf16[:])
         ident_f32 = const.tile([P, P], F32)
         make_identity(nc, ident_f32[:])
 
@@ -180,18 +177,25 @@ def tile_transformerconvblock_pa_t_kernel(
             return "vector" if turn["n"] % 2 == 0 else "scalar"
 
         def flip(n):
-            image = images[n // TILES_PER_IMAGE]
-            pixels = slice((n % TILES_PER_IMAGE) * P, (n % TILES_PER_IMAGE + 1) * P)
-            x_t = psum_fwd.tile([P, PLANES, P], BF16, name="x_t")
+            b, half = divmod(n, TILES_PER_IMAGE)
+            if half != 0:
+                return
+            banks = []
             for c in range(PASSES):
+                x_t = psum_fwd.tile([P, PACK, P], F32, name="x_t")
                 for t in range(PACK):
-                    nc.tensor.transpose(x_t[:, c * PACK + t, :], image[:, c, t, pixels], ident_bf16[:])
-            x_t_of[n] = x_t
+                    nc.tensor.transpose(x_t[:, t, :], images[b][:, c, t, :].bitcast(F32), ident_f32[:])
+                banks.append(x_t)
+            x_t_of[b] = banks
+
+        def flipped(n, c):
+            b, half = divmod(n, TILES_PER_IMAGE)
+            return x_t_of[b][c][:].rearrange("p t j -> p (t j)").bitcast(BF16).rearrange("p (j m) -> p m j", m=TILES_PER_IMAGE)[:, half, :]
 
         def measure(n, c):
             if c == 0:
                 stats_of[n] = small.tile([P, PASSES, 6], F32, name="stats")
-            nc.vector.bn_stats(out=stats_of[n][:, c, :], in_=x_t_of[n][:, c * PACK : (c + 1) * PACK, :])
+            nc.vector.bn_stats(out=stats_of[n][:, c, :], in_=flipped(n, c))
 
         def summarise(n):
             moments = small.tile([P, 2], F32, name="moments")
@@ -213,10 +217,12 @@ def tile_transformerconvblock_pa_t_kernel(
         def centre(n):
             affine = affine_of.pop(n)
             z = z_pool.tile([P, CHANNELS], F32, name="z")
-            nc.scalar.activation(
-                out=z[:], in_=x_t_of.pop(n)[:].rearrange("p g j -> p (g j)"), func=ACT.Identity,
-                bias=neg_ratio_of.pop(n)[:, 0:1], scale=affine[:, 0:1],
-            )
+            neg_ratio = neg_ratio_of.pop(n)
+            for c in range(PASSES):
+                nc.scalar.activation(
+                    out=z[:, c * PACK * P : (c + 1) * PACK * P], in_=flipped(n, c), func=ACT.Identity,
+                    bias=neg_ratio[:, 0:1], scale=affine[:, 0:1],
+                )
             z_of[n] = z
 
         def turn_back(j, g):
@@ -272,28 +278,37 @@ def tile_transformerconvblock_pa_t_kernel(
                 in_=grouped_of.pop((j, c))[:].rearrange("p w t -> p (w t)"),
             )
 
-        def multiply(n):
+        def accumulate(b, acc, half, cols):
+            codes, scales = mx_of[b]
+            pixels = slice(half * P, (half + 1) * P)
+            for c in range(PASSES):
+                nc.tensor.matmul_mx(
+                    out=acc,
+                    lhsT=codes[:, c, pixels].bitcast(FP8X4),
+                    lhsT_scale=scales[:, c, pixels],
+                    rhs=w_codes[:, c, cols].bitcast(FP8X4),
+                    rhs_scale=w_scales[:, c, cols],
+                    start=(c == 0),
+                    stop=(c == PASSES - 1),
+                )
+
+        def multiply_qk(n, spare=False):
             b, half = divmod(n, TILES_PER_IMAGE)
-            j, i = group_of[n]
-            codes, scales = mx_of[j]
-            pixels = slice(i * P, (i + 1) * P)
-            acc_qk_of[n] = psum_qk.tile([P, QK_COLS], F32, name="acc_qk")
-            if half == 0:
-                acc_v_of[b] = psum_v.tile([P, TILES_PER_IMAGE, HEAD_COLS], F32, name="acc_v")
-            for acc, cols in (
-                (acc_qk_of[n][:], slice(0, QK_COLS)),
-                (acc_v_of[b][:, half, :], slice(QK_COLS, OUT_COLS)),
-            ):
-                for c in range(PASSES):
-                    nc.tensor.matmul_mx(
-                        out=acc,
-                        lhsT=codes[:, c, pixels].bitcast(FP8X4),
-                        lhsT_scale=scales[:, c, pixels],
-                        rhs=w_codes[:, c, cols].bitcast(FP8X4),
-                        rhs_scale=w_scales[:, c, cols],
-                        start=(c == 0),
-                        stop=(c == PASSES - 1),
-                    )
+            if spare:
+                acc = psum_back.tile([P, QK_COLS], F32, name="z_t")
+            else:
+                acc = psum_acc.tile([P, QK_COLS], F32, name="acc")
+            accumulate(b, acc[:], half, slice(0, QK_COLS))
+            acc_qk_of[n] = acc
+
+        def multiply_v(b, spare=False):
+            if spare:
+                acc = psum_fwd.tile([P, TILES_PER_IMAGE, HEAD_COLS], F32, name="x_t")
+            else:
+                acc = psum_acc.tile([P, TILES_PER_IMAGE, HEAD_COLS], F32, name="acc")
+            for half in range(TILES_PER_IMAGE):
+                accumulate(b, acc[:, half, :], half, slice(QK_COLS, OUT_COLS))
+            acc_v_of[b] = acc
 
         def copy_out(dst, src, shared):
             if (DRAIN_COPY == 0 and helper(shared, "vector") == "vector") or (DRAIN_COPY == 1 and not shared):
@@ -310,83 +325,81 @@ def tile_transformerconvblock_pa_t_kernel(
         def empty_v(b, shared):
             copy_out(result_of[b][:, :, QK_COLS:OUT_COLS], acc_v_of.pop(b)[:], shared)
 
+        def empty(kind, n, shared):
+            if kind == "qk":
+                empty_qk(n, shared)
+            else:
+                empty_v(n, shared)
+                store(n)
+
         def store(b):
             result = result_of.pop(b)
             for o, out in enumerate(outs):
                 nc.sync.dma_start(
-                    out=out[b * PIXELS : (b + 1) * PIXELS, :].rearrange("(m p) n -> p m n", p=P),
+                    out=out[b * PIXELS : (b + 1) * PIXELS, :].rearrange("(p m) n -> p m n", p=P),
                     in_=result[:, :, o * HEAD_COLS : (o + 1) * HEAD_COLS],
                 )
 
-        backs = {}
-        gains = {}
-        packs = {}
-        quants = {}
-        mults = {}
-        empties = {}
-        next_mult = 0
-        for j, size in enumerate(GROUP_SIZES):
-            ready = first_of[j] + size - 1 + CENTRE_LAG
+        backs, gains, packs, quants, mults, copies = {}, {}, {}, {}, {}, {}
+        for b in range(IMAGES):
+            last = b == IMAGES - 1
+            ready = b * TILES_PER_IMAGE + TILES_PER_IMAGE - 1 + CENTRE_LAG
             for g in range(PLANES):
-                fast = LAST_FAST and j == len(GROUP_SIZES) - 1
-                s = ready + BACK_DELAY + (0 if fast else (g * size) // PLANES)
-                quant_delay = 1 if j >= len(GROUP_SIZES) - FAST_QUANTS else QUANT_DELAY
-                backs.setdefault(s, []).append((j, g))
-                gains.setdefault(s + GAIN_DELAY, []).append((j, g))
+                s = ready + 1 + (0 if last else g // PACK)
+                backs.setdefault(s, []).append((b, g))
+                gains.setdefault(s + 1, []).append((b, g))
                 if g % PACK == PACK - 1:
-                    packs.setdefault(s + GAIN_DELAY, []).append((j, g // PACK))
-                    quants.setdefault(s + GAIN_DELAY + quant_delay, []).append((j, g // PACK))
-            s = max(s + GAIN_DELAY + quant_delay + MULT_DELAY, next_mult)
-            for i in range(size):
-                mults.setdefault(s + i, []).append(first_of[j] + i)
-                empties.setdefault(s + i + EMPTY_DELAY, []).append(first_of[j] + i)
-            next_mult = s + size
+                    packs.setdefault(s + 1, []).append((b, g // PACK))
+            quants[ready + (3 if last else 4)] = b
+            x0 = ready + 5
+            x1 = x0 if last else x0 + 1
+            mults.setdefault(x0, []).append(("qk", b * TILES_PER_IMAGE, last))
+            mults.setdefault(x1, []).extend([("qk", b * TILES_PER_IMAGE + 1, last), ("v", b, last)])
+            copies.setdefault(x0 + 1, []).append(("qk", b * TILES_PER_IMAGE))
+            copies.setdefault(x1 + 1, []).extend([("qk", b * TILES_PER_IMAGE + 1), ("v", b)])
 
         def in_range(n):
             return 0 <= n < TILES
 
-        for slot in range(max(empties) + 1):
+        for slot in range(max(copies) + 1):
             shared = slot >= SHARE_FROM
+            shared_copy = slot >= COPY_SHARE_FROM
             slot_gains = gains.get(slot, [])
+            slot_copies = copies.get(slot, [])
             if in_range(slot - CENTRE_LAG):
                 root(slot - CENTRE_LAG)
-            for j, g in slot_gains[: (len(slot_gains) + 1) // 2]:
-                gain_and_shift(j, g, shared)
-            if MULT_POS == 0:
-                for n in mults.get(slot, []):
-                    multiply(n)
+            for b, g in slot_gains[: (len(slot_gains) + 1) // 2]:
+                gain_and_shift(b, g, shared)
             if in_range(slot):
                 flip(slot)
-            if MULT_POS == 1:
-                for n in mults.get(slot, []):
-                    multiply(n)
             if in_range(slot - MEASURE_LAG):
                 measure(slot - MEASURE_LAG, 0)
             if in_range(slot - CENTRE_LAG):
                 offset(slot - CENTRE_LAG)
             if in_range(slot - MEASURE_LAG):
                 measure(slot - MEASURE_LAG, 1)
-            for j, g in slot_gains[(len(slot_gains) + 1) // 2 :]:
-                gain_and_shift(j, g, shared)
+            for b, g in slot_gains[(len(slot_gains) + 1) // 2 :]:
+                gain_and_shift(b, g, shared)
             if in_range(slot - CENTRE_LAG):
                 centre(slot - CENTRE_LAG)
-            for j, g in backs.get(slot, []):
-                turn_back(j, g)
-            for n in empties.get(slot, []):
-                empty_qk(n, slot >= COPY_SHARE_FROM)
+            for b, g in backs.get(slot, []):
+                turn_back(b, g)
+            for kind, n in slot_copies[:1]:
+                empty(kind, n, shared_copy)
             if in_range(slot - MEASURE_LAG):
                 summarise(slot - MEASURE_LAG)
-            for j, c in quants.get(slot, []):
-                quantise(j, c)
-            for n in empties.get(slot, []):
-                if n % TILES_PER_IMAGE == TILES_PER_IMAGE - 1:
-                    empty_v(n // TILES_PER_IMAGE, slot >= COPY_SHARE_FROM)
-                    store(n // TILES_PER_IMAGE)
-            if MULT_POS == 2:
-                for n in mults.get(slot, []):
-                    multiply(n)
-            for j, c in packs.get(slot, []):
-                pack_words(j, c)
+            for kind, n in slot_copies[1:]:
+                empty(kind, n, shared_copy)
+            if slot in quants:
+                for c in range(PASSES):
+                    quantise(quants[slot], c)
+            for kind, n, spare in mults.get(slot, []):
+                if kind == "qk":
+                    multiply_qk(n, spare)
+                else:
+                    multiply_v(n, spare)
+            for b, c in packs.get(slot, []):
+                pack_words(b, c)
             if slot == GAIN_SLOT:
                 scale_gain_and_shift()
             if 0 <= slot - WPACK_SLOT < len(weights):

@@ -25,7 +25,7 @@ TILES = IMAGES * TILES_PER_IMAGE
 OUT_COLS = 3 * HEAD_COLS
 QK_COLS = 2 * HEAD_COLS
 EPS = 1e-5
-EARLY_IMAGES = 4
+LOAD_ORDER = ("image", "image", "weight", "image", "weight", "image", "vectors", "weight")
 
 GROUP_SIZES = (2,) * 16
 MAX_GROUP = max(GROUP_SIZES)
@@ -50,8 +50,8 @@ VECTOR_PLANES = ()
 SPLIT_IMAGES = 1
 FAST_QUANTS = 2
 GAIN_SLOT = 4
-WPACK_SLOT = 2
-WQUANT_SLOT = 5
+WPACK_SLOT = 1
+WQUANT_SLOT = 4
 
 FLOPS = 2 * IMAGES * PIXELS * CHANNELS * OUT_COLS
 
@@ -97,12 +97,18 @@ def tile_transformerconvblock_pa_t_kernel(
         gain_raw = const.tile([P, PASSES, PACK], BF16)
         shift_raw = const.tile([P, PASSES, PACK], BF16)
         mult_raw = const.tile([P, 1], BF16)
-        images = [load_image(b) for b in range(EARLY_IMAGES)]
-        nc.sync.dma_start(out=gain_raw[:], in_=ln1_w.rearrange("(c p t) -> p c t", c=PASSES, p=P))
-        nc.sync.dma_start(out=shift_raw[:], in_=ln1_b.rearrange("(c p t) -> p c t", c=PASSES, p=P))
-        nc.sync.dma_start(out=mult_raw[:], in_=scale_norm1.partition_broadcast(P))
-        w_raws = [load_weight(o) for o in range(len(weights))]
-        images.extend([load_image(b) for b in range(EARLY_IMAGES, IMAGES)])
+        images = []
+        w_raws = []
+        for step in LOAD_ORDER:
+            if step == "image":
+                images.append(load_image(len(images)))
+            elif step == "weight":
+                w_raws.append(load_weight(len(w_raws)))
+            else:
+                nc.sync.dma_start(out=gain_raw[:], in_=ln1_w.rearrange("(c p t) -> p c t", c=PASSES, p=P))
+                nc.sync.dma_start(out=shift_raw[:], in_=ln1_b.rearrange("(c p t) -> p c t", c=PASSES, p=P))
+                nc.sync.dma_start(out=mult_raw[:], in_=scale_norm1.partition_broadcast(P))
+        images.extend([load_image(b) for b in range(len(images), IMAGES)])
 
         warm = const.tile([P, 1], F32)
         nc.vector.memset(warm[:], 1.0)
@@ -168,13 +174,6 @@ def tile_transformerconvblock_pa_t_kernel(
         acc_qk_of = {}
         acc_v_of = {}
         result_of = {}
-        turn = {"n": 0}
-
-        def helper(shared, usual):
-            if not shared:
-                return usual
-            turn["n"] = turn["n"] + 1
-            return "vector" if turn["n"] % 2 == 0 else "scalar"
 
         def flip(n):
             b, half = divmod(n, TILES_PER_IMAGE)
@@ -225,11 +224,11 @@ def tile_transformerconvblock_pa_t_kernel(
                 )
             z_of[n] = z
 
-        def turn_back(j, g):
+        def turn_back(j, g, spare=False):
             size = GROUP_SIZES[j]
             per_bank = BANK_TILES // size
             if g % per_bank == 0:
-                if LAST_FAST and j == len(GROUP_SIZES) - 1 and (g // per_bank) % 2 == 1:
+                if spare:
                     bank_of[j] = psum_fwd.tile([P, per_bank, size, P], F32, name="x_t")
                 else:
                     bank_of[j] = psum_back.tile([P, per_bank, size, P], F32, name="z_t")
@@ -243,7 +242,7 @@ def tile_transformerconvblock_pa_t_kernel(
             if g == 0:
                 planes_of[j] = work.tile([P, PLANES, size * P], BF16, name="planes")
             z_t = z_t_of.pop((j, g)).rearrange("p m j -> p (m j)")
-            if g in VECTOR_PLANES or (shared and (g // (BANK_TILES // size)) % 2 == 1):
+            if shared:
                 nc.vector.tensor_scalar(
                     out=planes_of[j][:, g, :], in0=z_t, scalar1=gain[:, g : g + 1], scalar2=shift[:, g : g + 1],
                     op0=ALU.mult, op1=ALU.add,
@@ -253,9 +252,9 @@ def tile_transformerconvblock_pa_t_kernel(
                     out=planes_of[j][:, g, :], in_=z_t, func=ACT.Identity, bias=shift[:, g : g + 1], scale=gain[:, g : g + 1],
                 )
 
-        def pack_words(j, c):
+        def pack_words(j, c, on_vector=False):
             grouped = grouped_pool.tile([P, GROUP_SIZES[j] * P, PACK], BF16, name="grouped", align_bytes=64)
-            if j >= len(GROUP_SIZES) - LAST_PACK_V:
+            if on_vector:
                 nc.vector.tensor_copy(
                     out=grouped[:].rearrange("p (w i) t -> p w t i", i=4),
                     in_=planes_of[j][:, c * PACK : (c + 1) * PACK, :].rearrange("p t (w i) -> p w t i", i=4),
@@ -295,15 +294,17 @@ def tile_transformerconvblock_pa_t_kernel(
         def multiply_qk(n, spare=False):
             b, half = divmod(n, TILES_PER_IMAGE)
             if spare:
-                acc = psum_back.tile([P, QK_COLS], F32, name="z_t")
+                acc = psum_fwd.tile([P, QK_COLS], F32, name="x_t")
             else:
                 acc = psum_acc.tile([P, QK_COLS], F32, name="acc")
             accumulate(b, acc[:], half, slice(0, QK_COLS))
             acc_qk_of[n] = acc
 
-        def multiply_v(b, spare=False):
-            if spare:
+        def multiply_v(b, spare=False, final=False):
+            if final:
                 acc = psum_fwd.tile([P, TILES_PER_IMAGE, HEAD_COLS], F32, name="x_t")
+            elif spare:
+                acc = psum_back.tile([P, TILES_PER_IMAGE, HEAD_COLS], F32, name="z_t")
             else:
                 acc = psum_acc.tile([P, TILES_PER_IMAGE, HEAD_COLS], F32, name="acc")
             for half in range(TILES_PER_IMAGE):
@@ -311,7 +312,7 @@ def tile_transformerconvblock_pa_t_kernel(
             acc_v_of[b] = acc
 
         def copy_out(dst, src, shared):
-            if (DRAIN_COPY == 0 and helper(shared, "vector") == "vector") or (DRAIN_COPY == 1 and not shared):
+            if not shared:
                 nc.vector.tensor_copy(out=dst, in_=src)
             else:
                 nc.scalar.copy(out=dst, in_=src)
@@ -361,9 +362,9 @@ def tile_transformerconvblock_pa_t_kernel(
         def in_range(n):
             return 0 <= n < TILES
 
-        for slot in range(max(copies) + 1):
-            shared = slot >= SHARE_FROM
-            shared_copy = slot >= COPY_SHARE_FROM
+        for slot in range(TILES + 1):
+            shared = False
+            shared_copy = False
             slot_gains = gains.get(slot, [])
             slot_copies = copies.get(slot, [])
             if in_range(slot - CENTRE_LAG):
@@ -406,3 +407,59 @@ def tile_transformerconvblock_pa_t_kernel(
                 pack_weight(slot - WPACK_SLOT)
             if 0 <= slot - WQUANT_SLOT < len(weights):
                 quantise_weight(slot - WQUANT_SLOT)
+
+        V, S = False, True
+        root(31)
+        offset(31)
+        for g in (4, 5, 6, 7):
+            turn_back(14, g, True)
+        multiply_qk(25)
+        for g in (0, 1, 2, 3):
+            gain_and_shift(14, g, True)
+        pack_words(14, 0)
+        centre(31)
+        empty_qk(24, V)
+        for g in (0, 1, 2, 3):
+            turn_back(15, g)
+        multiply_v(12)
+        for g in (4, 5, 6, 7):
+            gain_and_shift(14, g, False)
+        quantise(13, 0)
+        quantise(13, 1)
+        for g in (4, 5, 6, 7):
+            turn_back(15, g, True)
+        empty_qk(25, V)
+        empty_v(12, V)
+        store(12)
+        multiply_qk(26)
+        for g in (0, 1, 2, 3):
+            gain_and_shift(15, g, False)
+        pack_words(14, 1, True)
+        quantise(14, 0)
+        quantise(14, 1)
+        multiply_qk(27)
+        multiply_v(13, True)
+        for g in (4, 5, 6, 7):
+            gain_and_shift(15, g, False)
+        pack_words(15, 0, True)
+        empty_qk(26, V)
+        multiply_qk(28, True)
+        multiply_qk(29, True)
+        multiply_v(14, True)
+        pack_words(15, 1, True)
+        empty_qk(27, S)
+        quantise(15, 0)
+        quantise(15, 1)
+        empty_v(13, S)
+        store(13)
+        multiply_qk(30)
+        multiply_qk(31)
+        empty_qk(28, S)
+        empty_qk(29, V)
+        multiply_v(15, True, True)
+        empty_v(14, S)
+        store(14)
+        empty_qk(30, V)
+        empty_qk(31, S)
+        empty_v(15, V)
+        store(15)

from contextlib import ExitStack

import concourse.mybir as mybir
from concourse.masks import make_identity

BF16 = mybir.dt.bfloat16
F32 = mybir.dt.float32
U32 = mybir.dt.uint32
U8 = mybir.dt.uint8
FP8X4 = mybir.dt.float8_e4m3fn_x4
ACT = mybir.ActivationFunctionType
ALU = mybir.AluOpType

P = 128
PACK = 4
K_PASS = P * PACK
IMAGES = 16
CHANNELS = 1024
PIXELS = 256
HEAD_COLS = 256
PASSES = CHANNELS // K_PASS
PLANES = PASSES * PACK
TILES_PER_IMAGE = PIXELS // P
TILES = IMAGES * TILES_PER_IMAGE
OUT_COLS = 3 * HEAD_COLS
QK_COLS = 2 * HEAD_COLS
EPS = 1e-5
LOAD_ORDER = ("image", "image", "weight", "image", "weight", "image", "vectors", "weight")

GROUP_SIZES = (2,) * 16
MAX_GROUP = max(GROUP_SIZES)
MEASURE_LAG = 1
CENTRE_LAG = 2
BACK_DELAY = 1
GAIN_DELAY = 1
QUANT_DELAY = 2
MULT_DELAY = 0
EMPTY_DELAY = 1
SHARE_FROM = 34
DRAIN_SPEED = 1
DRAIN_BANKS = 0
LAST_PACK_V = 1
PACK_PIXELS = 256
MULT_POS = 2
BANK_TILES = 4
LAST_FAST = 1
DRAIN_COPY = 0
COPY_SHARE_FROM = 34
VECTOR_PLANES = ()
SPLIT_IMAGES = 1
FAST_QUANTS = 2
GAIN_SLOT = 4
WPACK_SLOT = 1
WQUANT_SLOT = 4

FLOPS = 2 * IMAGES * PIXELS * CHANNELS * OUT_COLS


def tile_transformerconvblock_pa_t_kernel(
    tc, x, ln1_w, ln1_b, scale_norm1, W_Q, W_K, W_V, out_0, out_1, out_2
):
    nc = tc.nc
    weights = (W_Q, W_K, W_V)
    outs = [o.rearrange("b h w a d -> (b h w) (a d)") for o in (out_0, out_1, out_2)]

    with ExitStack() as stack:
        stack.enter_context(tc.manual_schedule())
        const = stack.enter_context(tc.tile_pool(name="const", bufs=1))
        image_pool = stack.enter_context(tc.tile_pool(name="image_pool", bufs=IMAGES))
        small = stack.enter_context(tc.tile_pool(name="small", bufs=4))
        z_pool = stack.enter_context(tc.tile_pool(name="z_pool", bufs=2 * MAX_GROUP + 2))
        work = stack.enter_context(tc.tile_pool(name="work", bufs=3))
        grouped_pool = stack.enter_context(tc.tile_pool(name="grouped_pool", bufs=2))
        result_pool = stack.enter_context(tc.tile_pool(name="result_pool", bufs=4))
        psum_fwd = stack.enter_context(tc.psum_pool(name="psum_fwd", bufs=4))
        psum_back = stack.enter_context(tc.psum_pool(name="psum_back", bufs=2))
        psum_acc = stack.enter_context(tc.psum_pool(name="psum_acc", bufs=2))

        def load_image(b):
            image = image_pool.tile([P, PASSES, PACK, PIXELS], BF16, name="image")
            source = x[b].rearrange("(c p t) h w -> p c (t h w)", c=PASSES, p=P)
            if b < SPLIT_IMAGES:
                for c in range(PASSES):
                    nc.sync.dma_start(out=image[:, c].rearrange("p t w -> p (t w)"), in_=source[:, c])
            else:
                nc.sync.dma_start(out=image[:].rearrange("p c t w -> p c (t w)"), in_=source)
            return image

        def load_weight(o):
            w_raw = const.tile([P, PASSES, PACK, HEAD_COLS], BF16, name="w_raw%d" % o)
            nc.sync.dma_start(
                out=w_raw[:].rearrange("p c t n -> p c (t n)"),
                in_=weights[o].rearrange("a r d -> (a r d)").rearrange("(c p tn) -> p c tn", c=PASSES, p=P),
            )
            return w_raw

        gain_raw = const.tile([P, PASSES, PACK], BF16)
        shift_raw = const.tile([P, PASSES, PACK], BF16)
        mult_raw = const.tile([P, 1], BF16)
        images = []
        w_raws = []
        for step in LOAD_ORDER:
            if step == "image":
                images.append(load_image(len(images)))
            elif step == "weight":
                w_raws.append(load_weight(len(w_raws)))
            else:
                nc.sync.dma_start(out=gain_raw[:], in_=ln1_w.rearrange("(c p t) -> p c t", c=PASSES, p=P))
                nc.sync.dma_start(out=shift_raw[:], in_=ln1_b.rearrange("(c p t) -> p c t", c=PASSES, p=P))
                nc.sync.dma_start(out=mult_raw[:], in_=scale_norm1.partition_broadcast(P))
        images.extend([load_image(b) for b in range(len(images), IMAGES)])

        warm = const.tile([P, 1], F32)
        nc.vector.memset(warm[:], 1.0)
        nc.scalar.activation(out=warm[:], in_=warm[:], func=ACT.Abs_reciprocal_sqrt, bias=0.0, scale=1.0)

        ident_f32 = const.tile([P, P], F32)
        make_identity(nc, ident_f32[:])

        mult = const.tile([P, 1], F32)
        gain = const.tile([P, PLANES], F32)
        shift = const.tile([P, PLANES], F32)

        def scale_gain_and_shift():
            nc.vector.tensor_copy(out=mult[:], in_=mult_raw[:])
            for scaled, raw in ((gain, gain_raw), (shift, shift_raw)):
                nc.vector.tensor_scalar(
                    out=scaled[:], in0=raw[:].rearrange("p c t -> p (c t)"),
                    scalar1=mult[:, 0:1], scalar2=None, op0=ALU.mult,
                )

        w_grouped = const.tile([P, PASSES, OUT_COLS, PACK], BF16, align_bytes=64)
        w_codes = const.tile([P, PASSES, OUT_COLS], U32, align_bytes=64)
        w_scales = const.tile([P, PASSES, OUT_COLS], U8, align_bytes=64)

        def interleave(dst, src):
            nc.gpsimd.tensor_scalar(
                out=dst, in0=src.rearrange("p t w -> p w t"), scalar1=1.0, scalar2=0.0, op0=ALU.mult, op1=ALU.add
            )

        def pack_weight(o):
            cols = slice(o * HEAD_COLS, (o + 1) * HEAD_COLS)
            for c in range(PASSES):
                interleave(w_grouped[:, c, cols, :], w_raws[o][:, c])

        def quantise_weight(o):
            cols = slice(o * HEAD_COLS, (o + 1) * HEAD_COLS)
            for c in range(PASSES):
                nc.vector.quantize_mx(
                    out=w_codes[:, c, cols].bitcast(FP8X4),
                    scales=w_scales[:, c, cols],
                    in_=w_grouped[:, c, cols, :].rearrange("p n t -> p (n t)"),
                )

        first_of = []
        for size in GROUP_SIZES:
            first_of.append(sum(GROUP_SIZES[: len(first_of)]))
        group_of = {}
        for j, size in enumerate(GROUP_SIZES):
            for i in range(size):
                group_of[first_of[j] + i] = (j, i)

        x_t_of = {}
        stats_of = {}
        moments_of = {}
        neg_ratio_of = {}
        affine_of = {}
        z_of = {}
        z_t_of = {}
        bank_of = {}
        planes_of = {}
        grouped_of = {}
        mx_of = {}
        acc_qk_of = {}
        acc_v_of = {}
        result_of = {}

        def flip(n):
            b, half = divmod(n, TILES_PER_IMAGE)
            if half != 0:
                return
            banks = []
            for c in range(PASSES):
                x_t = psum_fwd.tile([P, PACK, P], F32, name="x_t")
                for t in range(PACK):
                    nc.tensor.transpose(x_t[:, t, :], images[b][:, c, t, :].bitcast(F32), ident_f32[:])
                banks.append(x_t)
            x_t_of[b] = banks

        def flipped(n, c):
            b, half = divmod(n, TILES_PER_IMAGE)
            return x_t_of[b][c][:].rearrange("p t j -> p (t j)").bitcast(BF16).rearrange("p (j m) -> p m j", m=TILES_PER_IMAGE)[:, half, :]

        def measure(n, c):
            if c == 0:
                stats_of[n] = small.tile([P, PASSES, 6], F32, name="stats")
            nc.vector.bn_stats(out=stats_of[n][:, c, :], in_=flipped(n, c))

        def summarise(n):
            moments = small.tile([P, 2], F32, name="moments")
            nc.vector.bn_aggr(out=moments[:], in_=stats_of.pop(n)[:].rearrange("p c s -> p (c s)"))
            moments_of[n] = moments

        def root(n):
            affine = small.tile([P, 1], F32, name="affine")
            nc.scalar.activation(out=affine[:, 0:1], in_=moments_of[n][:, 1:2], func=ACT.Abs_reciprocal_sqrt, bias=EPS, scale=1.0)
            affine_of[n] = affine

        def offset(n):
            neg_ratio = small.tile([P, 1], F32, name="neg_ratio")
            nc.vector.tensor_scalar(
                out=neg_ratio[:], in0=moments_of.pop(n)[:, 0:1], scalar1=affine_of[n][:, 0:1], scalar2=-1.0, op0=ALU.mult, op1=ALU.mult
            )
            neg_ratio_of[n] = neg_ratio

        def centre(n):
            affine = affine_of.pop(n)
            z = z_pool.tile([P, CHANNELS], F32, name="z")
            neg_ratio = neg_ratio_of.pop(n)
            for c in range(PASSES):
                nc.scalar.activation(
                    out=z[:, c * PACK * P : (c + 1) * PACK * P], in_=flipped(n, c), func=ACT.Identity,
                    bias=neg_ratio[:, 0:1], scale=affine[:, 0:1],
                )
            z_of[n] = z

        def turn_back(j, g, spare=False):
            size = GROUP_SIZES[j]
            per_bank = BANK_TILES // size
            if g % per_bank == 0:
                if spare:
                    bank_of[j] = psum_fwd.tile([P, per_bank, size, P], F32, name="x_t")
                else:
                    bank_of[j] = psum_back.tile([P, per_bank, size, P], F32, name="z_t")
            z_t = bank_of[j][:, g % per_bank]
            for m in range(size):
                nc.tensor.transpose(z_t[:, m, :], z_of[first_of[j] + m][:, g * P : (g + 1) * P], ident_f32[:])
            z_t_of[j, g] = z_t

        def gain_and_shift(j, g, shared):
            size = GROUP_SIZES[j]
            if g == 0:
                planes_of[j] = work.tile([P, PLANES, size * P], BF16, name="planes")
            z_t = z_t_of.pop((j, g)).rearrange("p m j -> p (m j)")
            if shared:
                nc.vector.tensor_scalar(
                    out=planes_of[j][:, g, :], in0=z_t, scalar1=gain[:, g : g + 1], scalar2=shift[:, g : g + 1],
                    op0=ALU.mult, op1=ALU.add,
                )
            else:
                nc.scalar.activation(
                    out=planes_of[j][:, g, :], in_=z_t, func=ACT.Identity, bias=shift[:, g : g + 1], scale=gain[:, g : g + 1],
                )

        def pack_words(j, c, on_vector=False):
            grouped = grouped_pool.tile([P, GROUP_SIZES[j] * P, PACK], BF16, name="grouped", align_bytes=64)
            if on_vector:
                nc.vector.tensor_copy(
                    out=grouped[:].rearrange("p (w i) t -> p w t i", i=4),
                    in_=planes_of[j][:, c * PACK : (c + 1) * PACK, :].rearrange("p t (w i) -> p w t i", i=4),
                )
            else:
                for m in range(0, GROUP_SIZES[j] * P, PACK_PIXELS):
                    interleave(grouped[:, m : m + PACK_PIXELS, :], planes_of[j][:, c * PACK : (c + 1) * PACK, m : m + PACK_PIXELS])
            grouped_of[j, c] = grouped

        def quantise(j, c):
            size = GROUP_SIZES[j]
            if c == 0:
                codes = work.tile([P, PASSES, size * P], U32, name="codes", align_bytes=64)
                scales = work.tile([P, PASSES, size * P], U8, name="scales", align_bytes=64)
                mx_of[j] = (codes, scales)
            codes, scales = mx_of[j]
            nc.vector.quantize_mx(
                out=codes[:, c, :].bitcast(FP8X4),
                scales=scales[:, c, :],
                in_=grouped_of.pop((j, c))[:].rearrange("p w t -> p (w t)"),
            )

        def accumulate(b, acc, half, cols):
            codes, scales = mx_of[b]
            pixels = slice(half * P, (half + 1) * P)
            for c in range(PASSES):
                nc.tensor.matmul_mx(
                    out=acc,
                    lhsT=codes[:, c, pixels].bitcast(FP8X4),
                    lhsT_scale=scales[:, c, pixels],
                    rhs=w_codes[:, c, cols].bitcast(FP8X4),
                    rhs_scale=w_scales[:, c, cols],
                    start=(c == 0),
                    stop=(c == PASSES - 1),
                )

        def multiply_qk(n, spare=False):
            b, half = divmod(n, TILES_PER_IMAGE)
            if spare:
                acc = psum_fwd.tile([P, QK_COLS], F32, name="x_t")
            else:
                acc = psum_acc.tile([P, QK_COLS], F32, name="acc")
            accumulate(b, acc[:], half, slice(0, QK_COLS))
            acc_qk_of[n] = acc

        def multiply_v(b, spare=False, final=False):
            if final:
                acc = psum_fwd.tile([P, TILES_PER_IMAGE, HEAD_COLS], F32, name="x_t")
            elif spare:
                acc = psum_back.tile([P, TILES_PER_IMAGE, HEAD_COLS], F32, name="z_t")
            else:
                acc = psum_acc.tile([P, TILES_PER_IMAGE, HEAD_COLS], F32, name="acc")
            for half in range(TILES_PER_IMAGE):
                accumulate(b, acc[:, half, :], half, slice(QK_COLS, OUT_COLS))
            acc_v_of[b] = acc

        def copy_out(dst, src, shared):
            if not shared:
                nc.vector.tensor_copy(out=dst, in_=src)
            else:
                nc.scalar.copy(out=dst, in_=src)

        def empty_qk(n, shared):
            b, half = divmod(n, TILES_PER_IMAGE)
            if half == 0:
                result_of[b] = result_pool.tile([P, TILES_PER_IMAGE, OUT_COLS], F32, name="result")
            copy_out(result_of[b][:, half, 0:QK_COLS], acc_qk_of.pop(n)[:], shared)

        def empty_v(b, shared):
            copy_out(result_of[b][:, :, QK_COLS:OUT_COLS], acc_v_of.pop(b)[:], shared)

        def empty(kind, n, shared):
            if kind == "qk":
                empty_qk(n, shared)
            else:
                empty_v(n, shared)
                store(n)

        def store(b):
            result = result_of.pop(b)
            for o, out in enumerate(outs):
                nc.sync.dma_start(
                    out=out[b * PIXELS : (b + 1) * PIXELS, :].rearrange("(p m) n -> p m n", p=P),
                    in_=result[:, :, o * HEAD_COLS : (o + 1) * HEAD_COLS],
                )

        backs, gains, packs, quants, mults, copies = {}, {}, {}, {}, {}, {}
        for b in range(IMAGES):
            last = b == IMAGES - 1
            ready = b * TILES_PER_IMAGE + TILES_PER_IMAGE - 1 + CENTRE_LAG
            for g in range(PLANES):
                s = ready + 1 + (0 if last else g // PACK)
                backs.setdefault(s, []).append((b, g))
                gains.setdefault(s + 1, []).append((b, g))
                if g % PACK == PACK - 1:
                    packs.setdefault(s + 1, []).append((b, g // PACK))
            quants[ready + (3 if last else 4)] = b
            x0 = ready + 5
            x1 = x0 if last else x0 + 1
            mults.setdefault(x0, []).append(("qk", b * TILES_PER_IMAGE, last))
            mults.setdefault(x1, []).extend([("qk", b * TILES_PER_IMAGE + 1, last), ("v", b, last)])
            copies.setdefault(x0 + 1, []).append(("qk", b * TILES_PER_IMAGE))
            copies.setdefault(x1 + 1, []).extend([("qk", b * TILES_PER_IMAGE + 1), ("v", b)])

        def in_range(n):
            return 0 <= n < TILES

        for slot in range(TILES + 1):
            shared = False
            shared_copy = False
            slot_gains = gains.get(slot, [])
            slot_copies = copies.get(slot, [])
            if in_range(slot - CENTRE_LAG):
                root(slot - CENTRE_LAG)
            for b, g in slot_gains[: (len(slot_gains) + 1) // 2]:
                gain_and_shift(b, g, shared)
            if in_range(slot):
                flip(slot)
            if in_range(slot - MEASURE_LAG):
                measure(slot - MEASURE_LAG, 0)
            if in_range(slot - CENTRE_LAG):
                offset(slot - CENTRE_LAG)
            if in_range(slot - MEASURE_LAG):
                measure(slot - MEASURE_LAG, 1)
            for b, g in slot_gains[(len(slot_gains) + 1) // 2 :]:
                gain_and_shift(b, g, shared)
            if in_range(slot - CENTRE_LAG):
                centre(slot - CENTRE_LAG)
            for b, g in backs.get(slot, []):
                turn_back(b, g)
            for kind, n in slot_copies[:1]:
                empty(kind, n, shared_copy)
            if in_range(slot - MEASURE_LAG):
                summarise(slot - MEASURE_LAG)
            for kind, n in slot_copies[1:]:
                empty(kind, n, shared_copy)
            if slot in quants:
                for c in range(PASSES):
                    quantise(quants[slot], c)
            for kind, n, spare in mults.get(slot, []):
                if kind == "qk":
                    multiply_qk(n, spare)
                else:
                    multiply_v(n, spare)
            for b, c in packs.get(slot, []):
                pack_words(b, c)
            if slot == GAIN_SLOT:
                scale_gain_and_shift()
            if 0 <= slot - WPACK_SLOT < len(weights):
                pack_weight(slot - WPACK_SLOT)
            if 0 <= slot - WQUANT_SLOT < len(weights):
                quantise_weight(slot - WQUANT_SLOT)

        V, S = False, True
        root(31)
        offset(31)
        for g in (4, 5, 6, 7):
            turn_back(14, g, True)
        multiply_qk(25)
        for g in (0, 1, 2, 3):
            gain_and_shift(14, g, True)
        pack_words(14, 0)
        centre(31)
        empty_qk(24, V)
        for g in (0, 1, 2, 3):
            turn_back(15, g)
        multiply_v(12)
        for g in (4, 5, 6, 7):
            gain_and_shift(14, g, False)
        quantise(13, 0)
        quantise(13, 1)
        for g in (4, 5, 6, 7):
            turn_back(15, g, True)
        empty_qk(25, V)
        empty_v(12, V)
        store(12)
        multiply_qk(26)
        for g in (0, 1, 2, 3):
            gain_and_shift(15, g, False)
        pack_words(14, 1, True)
        quantise(14, 0)
        quantise(14, 1)
        multiply_qk(27)
        multiply_v(13, True)
        for g in (4, 5, 6, 7):
            gain_and_shift(15, g, False)
        pack_words(15, 0, True)
        empty_qk(26, V)
        multiply_qk(28, True)
        multiply_qk(29, True)
        multiply_v(14, True)
        pack_words(15, 1, True)
        empty_qk(27, S)
        quantise(15, 0)
        quantise(15, 1)
        empty_v(13, S)
        store(13)
        multiply_qk(30)
        multiply_qk(31)
        empty_qk(28, S)
        empty_qk(29, V)
        multiply_v(15, True, True)
        empty_v(14, S)
        store(14)
        empty_qk(30, V)
        empty_qk(31, S)
        empty_v(15, V)
        store(15)
